import numpy as np
import ml_dtypes


def mxq(x, axis, fmt="e4m3"):
    dtype, down = {"e4m3": (ml_dtypes.float8_e4m3fn, 7), "e5m2": (ml_dtypes.float8_e5m2, 14)}[fmt]
    v = np.moveaxis(np.asarray(x, np.float32).astype(ml_dtypes.bfloat16).astype(np.float64), axis, -1)
    blocks = v.reshape(v.shape[:-1] + (-1, 32))
    amax = np.abs(blocks).max(-1, keepdims=True)
    byte = np.maximum(np.where(amax > 0, np.frexp(amax)[1] - 1 + 127, 0) - down, 1)
    scale = np.exp2(byte - 127.0)
    codes = (blocks / scale).astype(np.float32).astype(dtype).astype(np.float64)
    return np.moveaxis((codes * scale).reshape(v.shape), -1, axis)


WIDE = False


def mx_kscale(k):
    if not WIDE:
        return np.ones(k)
    levels = np.array([10, -10, 5, -5, 0])
    a = np.random.permutation(np.resize(levels, k // 512 * 4)).reshape(k // 512, 4)
    idx = np.arange(k)
    return np.exp2(a[idx // 512, idx % 128 // 32])


BF16 = ml_dtypes.bfloat16


def bf(x):
    return np.asarray(x, np.float32).astype(BF16)


def f64(x):
    return np.asarray(x).astype(np.float64)


B, M, C, HD, H, W = 2, 4, 512, 512, 16, 16
SHIFTS = [(0, 0)] + [(r, c) for r in (-1, 0, 1) for c in (-1, 0, 1) if (r, c) != (0, 0)]
NS = len(SHIFTS)
K1 = NS * C


def moved(v, r, c):
    p = np.pad(v, ((0, 0), (0, 0), (1, 1), (1, 1)))
    return p[:, :, r + 1:r + 1 + H, c + 1:c + 1 + W]


def setup_inputs():
    t = mx_kscale(HD)
    return {"x": bf(np.random.standard_normal((B, M * C, H, W))),
            "w1": bf(np.random.standard_normal((M, HD, K1)) / np.sqrt(K1) * t[None, :, None]),
            "b1": bf(np.random.standard_normal(M * HD) * 0.3 * np.tile(t, M)),
            "w2": bf(np.random.standard_normal((M, C, HD)) * 1.5 / np.sqrt(HD) / t[None, None, :]),
            "b2": bf(np.random.standard_normal(M * C) * 0.3)}


def reference(x, w1, b1, w2, b2):
    x = f64(x)
    xq = mxq(x, 1, "e4m3").reshape(B, M, C, H * W)
    w1q = mxq(f64(w1), 2, "e4m3").reshape(M, HD, NS, C)
    pre = []
    for m in range(M):
        acc = 0.0
        for j in range(NS):
            g = m * NS + j
            r, c = SHIFTS[g // M]
            y = w1q[m, :, j] @ xq[:, g % M]
            acc = acc + moved(y.reshape(B, HD, H, W), r, c)
        pre.append(acc)
    hdn = np.maximum(np.stack(pre, axis=1).reshape(B, M, HD, H * W) + f64(b1).reshape(1, M, HD, 1), 0.0)
    dx = (mxq(f64(w2), 2, "e4m3")[None] @ mxq(hdn, 2, "e4m3")) + f64(b2).reshape(1, M, C, 1)
    return x + dx.reshape(B, M * C, H, W)

@@ -1,0 +1,292 @@
+from contextlib import ExitStack
+
+import concourse.mybir as mybir
+from concourse.masks import make_identity
+
+BF16 = mybir.dt.bfloat16
+F32 = mybir.dt.float32
+I32 = mybir.dt.int32
+U32 = mybir.dt.uint32
+U8 = mybir.dt.uint8
+FP8X4 = mybir.dt.float8_e4m3fn_x4
+ADD = mybir.AluOpType.add
+RELU = mybir.ActivationFunctionType.Relu
+
+P = 128
+PACK = 4
+STRETCH = P * PACK
+WORDS = STRETCH // 2
+
+BATCH, GROUPS, GRID = 2, 4, 16
+PIXELS = GRID * GRID
+COLS = BATCH * PIXELS
+ROW = BATCH * GRID
+PADDED = COLS + 2 * ROW
+SHIFTS = [(0, 0)] + [(r, c) for r in (-1, 0, 1) for c in (-1, 0, 1) if (r, c) != (0, 0)]
+NS = len(SHIFTS)
+TILES = STRETCH // P
+UNITS = GROUPS * TILES
+BLOCKS = NS + 1
+AHEAD = 2
+RAW_BUFS = 4
+
+FLOPS = 2 * COLS * GROUPS * STRETCH * (NS * STRETCH + STRETCH)
+
+
+def tile_parallelnca_pa_kernel(tc, x, w1, b1, w2, b2, out):
+    nc = tc.nc
+
+    x_rows = x.rearrange("n (g u q e) h w -> g n q u (e h w)", g=GROUPS, u=2, e=2)
+    w1_rows = w1.rearrange("m (u p e) k -> m u e p k", u=2, e=2)
+    w2_rows = w2.rearrange("m (u p e) k -> m p u (e k)", u=2, e=2)
+    out_rows = out.rearrange("n (m u p e) h w -> m u p n (e h w)", m=GROUPS, u=2, e=2)
+
+    with ExitStack() as ctx:
+        keep = ctx.enter_context(tc.tile_pool(name="keep", bufs=1))
+        x_pool = ctx.enter_context(tc.tile_pool(name="x_pool", bufs=GROUPS))
+        raw_pool = ctx.enter_context(tc.tile_pool(name="raw_pool", bufs=RAW_BUFS))
+        pair_pool = ctx.enter_context(tc.tile_pool(name="pair_pool", bufs=2))
+        code_pool = ctx.enter_context(tc.tile_pool(name="code_pool", bufs=AHEAD + 1))
+        out_pool = ctx.enter_context(tc.tile_pool(name="out_pool", bufs=3))
+        turn_psum = ctx.enter_context(tc.psum_pool(name="turn_psum", bufs=BLOCKS // 2))
+        acc_psum = ctx.enter_context(tc.psum_pool(name="acc_psum", bufs=3))
+        ctx.enter_context(tc.manual_schedule())
+
+        identity = keep.tile([P, P], F32, name="identity")
+        bias_rows = keep.tile([P, 2 * P], BF16, name="bias_rows")
+        bias = keep.tile([P, 2 * UNITS], F32, name="bias")
+        x_raw = keep.tile([P, BATCH, GROUPS, PACK, PIXELS], BF16, name="x_raw")
+        x_centre = keep.tile([P, GROUPS, GRID * BATCH, GRID, PACK], BF16, name="x_centre", align_bytes=64)
+        x_codes = keep.tile([P, 3, GROUPS, PADDED], U32, name="x_codes", align_bytes=64)
+        x_scales = keep.tile([P, 3, GROUPS, COLS], U8, name="x_scales", align_bytes=64)
+        x_scales_padded = keep.tile([P, 3, GROUPS, PADDED], U8, name="x_scales_padded", align_bytes=64)
+        w2_codes = keep.tile([P, GROUPS, STRETCH], U32, name="w2_codes", align_bytes=64)
+        w2_scales = keep.tile([P, GROUPS, STRETCH], U8, name="w2_scales", align_bytes=64)
+
+        make_identity(nc, identity[:])
+        nc.vector.memset(bias_rows[:], 0.0)
+        nc.vector.memset(x_scales[:].bitcast(I32), 0)
+        nc.vector.memset(x_scales_padded[:].bitcast(I32), 0)
+        nc.vector.memset(x_codes[:, :, :, 0:ROW].bitcast(I32), 0)
+        nc.vector.memset(x_codes[:, :, :, ROW + COLS : PADDED].bitcast(I32), 0)
+
+        def load_x(g):
+            for n in range(BATCH):
+                nc.sync.dma_start(
+                    out=x_raw[:, n, g].rearrange("q (u e) f -> q u (e f)", u=2),
+                    in_=x_rows[g, n],
+                )
+
+        def regroup_x(g):
+            grouped = x_centre[:, g].rearrange("q (i n) j t -> q i n j t", n=BATCH)
+            for n, copy in ((0, nc.vector.tensor_copy), (1, nc.scalar.copy)):
+                copy(
+                    out=grouped[:, :, n],
+                    in_=x_raw[:, n, g].rearrange("q t (i j) -> q i j t", j=GRID),
+                )
+
+        def shift_x(c, g):
+            shifted = x_pool.tile([P, GRID * BATCH, GRID, PACK], BF16, tag="x_shifted", align_bytes=64)
+            first, last = max(0, -c), GRID - max(0, c)
+            nc.vector.tensor_copy(
+                out=shifted[:, :, first:last, :],
+                in_=x_centre[:, g, :, first + c : last + c, :],
+            )
+            border = 0 if c < 0 else GRID - 1
+            nc.vector.memset(shifted[:, :, border, :], 0.0)
+            return shifted[:]
+
+        def quantise_x(c, g, grouped):
+            nc.vector.quantize_mx(
+                out=x_codes[:, c + 1, g, ROW : ROW + COLS].bitcast(FP8X4),
+                scales=x_scales[:, c + 1, g, :],
+                in_=grouped.rearrange("q a j t -> q (a j t)"),
+            )
+
+        def pad_x_scales(c):
+            nc.vector.tensor_copy(
+                out=x_scales_padded[:, c + 1, :, ROW : ROW + COLS].bitcast(I32),
+                in_=x_scales[:, c + 1].bitcast(I32),
+            )
+
+        w1_raw = {}
+        w2_raw = {}
+        w_grouped = {}
+        w1_codes = {}
+        w1_scales = {}
+
+        def load_unit(k):
+            m, t = divmod(k, TILES)
+            u, e = divmod(t, 2)
+            w1_raw[k] = raw_pool.tile([P, NS * STRETCH], BF16, name="w1_raw", tag="w1_raw")
+            nc.sync.dma_start(out=w1_raw[k][:], in_=w1_rows[m, u, e])
+            if t == 0:
+                w2_raw[m] = pair_pool.tile([P, TILES, STRETCH], BF16, name="w2_raw", tag="w2_raw")
+                nc.sync.dma_start(
+                    out=w2_raw[m][:].rearrange("p (u e) k -> p u (e k)", u=2), in_=w2_rows[m]
+                )
+
+        def transpose_unit(k):
+            m, t = divmod(k, TILES)
+            words = w1_raw[k][:].bitcast(F32)
+            blocks = [words[:, WORDS * j : WORDS * (j + 1)] for j in range(NS)]
+            blocks.append(w2_raw[m][:, t, :].bitcast(F32))
+            w_grouped[k] = pair_pool.tile(
+                [P, BLOCKS * STRETCH], BF16, name="w_grouped", tag="w_grouped", align_bytes=64
+            )
+            grouped_words = w_grouped[k][:].bitcast(F32).rearrange("p (b r u) -> p b r u", r=P, u=2)
+            for first in range(0, BLOCKS, 2):
+                bank = turn_psum.tile([P, 2, 2, P], F32, tag="turned")
+                for a in range(2):
+                    for u in range(2):
+                        nc.tensor.transpose(
+                            bank[:, a, u, :], blocks[first + a][:, P * u : P * (u + 1)], identity[:]
+                        )
+                nc.scalar.copy(
+                    out=grouped_words[:, first : first + 2],
+                    in_=bank[:].rearrange("p a u r -> p a r u"),
+                )
+
+        def quantise_unit(k):
+            m, t = divmod(k, TILES)
+            w1_codes[k] = code_pool.tile([P, NS * P], U32, name="w1_codes", tag="w1_codes", align_bytes=64)
+            w1_scales[k] = code_pool.tile([P, NS * P], U8, name="w1_scales", tag="w1_scales", align_bytes=64)
+            for lo, hi in ((0, NS - 1), (NS - 1, NS)):
+                nc.vector.quantize_mx(
+                    out=w1_codes[k][:, P * lo : P * hi].bitcast(FP8X4),
+                    scales=w1_scales[k][:, P * lo : P * hi],
+                    in_=w_grouped[k][:, STRETCH * lo : STRETCH * hi],
+                )
+            nc.vector.quantize_mx(
+                out=w2_codes[:, m, P * t : P * (t + 1)].bitcast(FP8X4),
+                scales=w2_scales[:, m, P * t : P * (t + 1)],
+                in_=w_grouped[k][:, STRETCH * NS : STRETCH * BLOCKS],
+            )
+
+        hidden = {}
+        hidden_codes = {}
+        hidden_scales = {}
+        out_tiles = {}
+
+        def first_product(k):
+            m, t = divmod(k, TILES)
+            acc = acc_psum.tile([P, COLS], F32, tag="acc")
+            for j in range(NS):
+                copy_number, g = divmod(m * NS + j, GROUPS)
+                r, c = SHIFTS[copy_number]
+                window = slice(ROW * (1 + r), ROW * (1 + r) + COLS)
+                if r == 0:
+                    rhs_scale = x_scales[:, c + 1, g, :]
+                else:
+                    rhs_scale = x_scales_padded[:, c + 1, g, window]
+                nc.tensor.matmul_mx(
+                    out=acc[:],
+                    lhsT=w1_codes[k][:, P * j : P * (j + 1)].bitcast(FP8X4),
+                    lhsT_scale=w1_scales[k][:, P * j : P * (j + 1)],
+                    rhs=x_codes[:, c + 1, g, window].bitcast(FP8X4),
+                    rhs_scale=rhs_scale,
+                    start=(j == 0),
+                    stop=(j == NS - 1),
+                )
+            if t == 0:
+                hidden[m] = pair_pool.tile([P, TILES, COLS], BF16, name="hidden", tag="hidden")
+            nc.scalar.activation(
+                out=hidden[m][:, t, :].rearrange("p (n i j) -> p n i j", n=BATCH, j=GRID),
+                in_=acc[:].rearrange("p (i n j) -> p n i j", n=BATCH, j=GRID),
+                func=RELU,
+                bias=bias[:, k : k + 1],
+                scale=1.0,
+            )
+
+        def quantise_hidden(m):
+            grouped = pair_pool.tile([P, COLS, PACK], BF16, tag="hidden_grouped", align_bytes=64)
+            nc.vector.tensor_copy(
+                out=grouped[:].rearrange("p (c i) t -> p c t i", i=4),
+                in_=hidden[m][:].rearrange("p t (c i) -> p c t i", i=4),
+            )
+            hidden_codes[m] = pair_pool.tile([P, COLS], U32, name="hidden_codes", tag="hidden_codes", align_bytes=64)
+            hidden_scales[m] = pair_pool.tile([P, COLS], U8, name="hidden_scales", tag="hidden_scales", align_bytes=64)
+            nc.vector.quantize_mx(
+                out=hidden_codes[m][:].bitcast(FP8X4),
+                scales=hidden_scales[m][:],
+                in_=grouped[:].rearrange("p w t -> p (w t)"),
+            )
+
+        def second_product(m, t):
+            u, e = divmod(t, 2)
+            acc = acc_psum.tile([P, COLS], F32, tag="acc")
+            nc.tensor.matmul_mx(
+                out=acc[:],
+                lhsT=w2_codes[:, m, P * t : P * (t + 1)].bitcast(FP8X4),
+                lhsT_scale=w2_scales[:, m, P * t : P * (t + 1)],
+                rhs=hidden_codes[m][:].bitcast(FP8X4),
+                rhs_scale=hidden_scales[m][:],
+                start=True,
+                stop=True,
+            )
+            if e == 0:
+                out_tiles[m, u] = out_pool.tile([P, BATCH, 2, PIXELS], F32, name="out_tile", tag="out_tile")
+            nc.vector.scalar_tensor_tensor(
+                out=out_tiles[m, u][:, :, e, :],
+                in0=acc[:].rearrange("p (n f) -> p n f", n=BATCH),
+                scalar=bias[:, UNITS + TILES * m + t : UNITS + TILES * m + t + 1],
+                in1=x_raw[:, :, m, t, :],
+                op0=ADD,
+                op1=ADD,
+            )
+            if e == 1:
+                nc.sync.dma_start(
+                    out=out_rows[m, u], in_=out_tiles[m, u][:].rearrange("p n e f -> p n (e f)")
+                )
+
+        for g in range(GROUPS):
+            load_x(g)
+        load_unit(0)
+        nc.sync.dma_start(out=bias_rows[0:8, :], in_=b1.rearrange("(r c) -> r c", c=2 * P))
+        nc.sync.dma_start(out=bias_rows[8:16, :], in_=b2.rearrange("(r c) -> r c", c=2 * P))
+        for k in range(1, RAW_BUFS):
+            load_unit(k)
+
+        left = {}
+        for g in range(GROUPS + 1):
+            if g < GROUPS:
+                regroup_x(g)
+            if g > 0:
+                quantise_x(0, g - 1, x_centre[:, g - 1])
+                left[g - 1] = shift_x(-1, g - 1)
+        pad_x_scales(0)
+
+        transpose_unit(0)
+        load_unit(RAW_BUFS)
+        bias_bank = turn_psum.tile([P, 2, 2, P], F32, tag="turned")
+        nc.tensor.transpose(bias_bank[:, 0, 0, :], bias_rows[:].bitcast(F32), identity[:])
+        nc.vector.tensor_copy(out=bias[:], in_=bias_bank[:, 0, 0, 0:UNITS].bitcast(BF16))
+        quantise_unit(0)
+        for g in range(GROUPS):
+            quantise_x(-1, g, left[g])
+        pad_x_scales(-1)
+        transpose_unit(1)
+        load_unit(RAW_BUFS + 1)
+        quantise_unit(1)
+
+        for k in range(UNITS):
+            m, t = divmod(k, TILES)
+            if k + AHEAD < UNITS:
+                transpose_unit(k + AHEAD)
+            if k + AHEAD + RAW_BUFS < UNITS:
+                load_unit(k + AHEAD + RAW_BUFS)
+            if m == 0:
+                right = shift_x(1, t)
+            if k + AHEAD < UNITS:
+                quantise_unit(k + AHEAD)
+            if m == 0:
+                quantise_x(1, t, right)
+            first_product(k)
+            if m > 0:
+                second_product(m - 1, t)
+            if t == TILES - 1:
+                quantise_hidden(m)
+                if m == 0:
+                    pad_x_scales(1)
+        for t in range(TILES):
+            second_product(GROUPS - 1, t)

@@ -26,9 +26,18 @@ SHIFTS = [(0, 0)] + [(r, c) for r in (-1, 0, 1) for c in (-1, 0, 1) if (r, c) !=
 NS = len(SHIFTS)
 TILES = STRETCH // P
 UNITS = GROUPS * TILES
-BLOCKS = NS + 1
+BANKS = 5
+FIRST_W2 = 3
 AHEAD = 2
+BEFORE = NS // 2
 RAW_BUFS = 4
+
+
+def w2_tiles(k):
+    return [i for i in range(UNITS) if max(FIRST_W2 + i // 2, i) == k]
+
+
+MAX_BLOCKS = NS + max(len(w2_tiles(k)) for k in range(UNITS))
 
 FLOPS = 2 * COLS * GROUPS * STRETCH * (NS * STRETCH + STRETCH)
 
@@ -43,12 +52,11 @@ def tile_parallelnca_pa_kernel(tc, x, w1, b1, w2, b2, out):
 
     with ExitStack() as ctx:
         keep = ctx.enter_context(tc.tile_pool(name="keep", bufs=1))
-        x_pool = ctx.enter_context(tc.tile_pool(name="x_pool", bufs=GROUPS))
         raw_pool = ctx.enter_context(tc.tile_pool(name="raw_pool", bufs=RAW_BUFS))
         pair_pool = ctx.enter_context(tc.tile_pool(name="pair_pool", bufs=2))
         code_pool = ctx.enter_context(tc.tile_pool(name="code_pool", bufs=AHEAD + 1))
         out_pool = ctx.enter_context(tc.tile_pool(name="out_pool", bufs=3))
-        turn_psum = ctx.enter_context(tc.psum_pool(name="turn_psum", bufs=BLOCKS // 2))
+        turn_psum = ctx.enter_context(tc.psum_pool(name="turn_psum", bufs=BANKS))
         acc_psum = ctx.enter_context(tc.psum_pool(name="acc_psum", bufs=3))
         ctx.enter_context(tc.manual_schedule())
 
@@ -63,12 +71,19 @@ def tile_parallelnca_pa_kernel(tc, x, w1, b1, w2, b2, out):
         w2_codes = keep.tile([P, GROUPS, STRETCH], U32, name="w2_codes", align_bytes=64)
         w2_scales = keep.tile([P, GROUPS, STRETCH], U8, name="w2_scales", align_bytes=64)
 
+        def x_words(c, lo, hi):
+            words = x_codes[:, c + 1, lo:hi, ROW : ROW + COLS].bitcast(I32)
+            return words.rearrange("q g (a j) -> q g a j", j=GRID)
+
         make_identity(nc, identity[:])
         nc.vector.memset(bias_rows[:], 0.0)
-        nc.vector.memset(x_scales[:].bitcast(I32), 0)
+        nc.vector.memset(x_scales[:, 1].bitcast(I32), 0)
         nc.vector.memset(x_scales_padded[:].bitcast(I32), 0)
         nc.vector.memset(x_codes[:, :, :, 0:ROW].bitcast(I32), 0)
         nc.vector.memset(x_codes[:, :, :, ROW + COLS : PADDED].bitcast(I32), 0)
+        for c in (-1, 1):
+            border = 0 if c < 0 else GRID - 1
+            nc.vector.memset(x_words(c, 0, GROUPS)[:, :, :, border], 0)
 
         def load_x(g):
             for n in range(BATCH):
@@ -85,28 +100,36 @@ def tile_parallelnca_pa_kernel(tc, x, w1, b1, w2, b2, out):
                     in_=x_raw[:, n, g].rearrange("q t (i j) -> q i j t", j=GRID),
                 )
 
-        def shift_x(c, g):
-            shifted = x_pool.tile([P, GRID * BATCH, GRID, PACK], BF16, tag="x_shifted", align_bytes=64)
+        def quantise_x(g):
+            nc.vector.quantize_mx(
+                out=x_codes[:, 1, g, ROW : ROW + COLS].bitcast(FP8X4),
+                scales=x_scales[:, 1, g, :],
+                in_=x_centre[:, g].rearrange("q a j t -> q (a j t)"),
+            )
+
+        def shift_words(c, lo, hi):
             first, last = max(0, -c), GRID - max(0, c)
             nc.vector.tensor_copy(
-                out=shifted[:, :, first:last, :],
-                in_=x_centre[:, g, :, first + c : last + c, :],
-            )
-            border = 0 if c < 0 else GRID - 1
-            nc.vector.memset(shifted[:, :, border, :], 0.0)
-            return shifted[:]
-
-        def quantise_x(c, g, grouped):
-            nc.vector.quantize_mx(
-                out=x_codes[:, c + 1, g, ROW : ROW + COLS].bitcast(FP8X4),
-                scales=x_scales[:, c + 1, g, :],
-                in_=grouped.rearrange("q a j t -> q (a j t)"),
+                out=x_words(c, lo, hi)[:, :, :, first:last],
+                in_=x_words(0, lo, hi)[:, :, :, first + c : last + c],
             )
 
-        def pad_x_scales(c):
+        def shift_scales(c):
             nc.vector.tensor_copy(
-                out=x_scales_padded[:, c + 1, :, ROW : ROW + COLS].bitcast(I32),
-                in_=x_scales[:, c + 1].bitcast(I32),
+                out=x_scales_padded[:, c + 1, :, ROW - c : ROW - c + COLS],
+                in_=x_scales[:, 1],
+            )
+
+        def pad_x_scales():
+            nc.vector.tensor_copy(
+                out=x_scales_padded[:, 1, :, ROW : ROW + COLS].bitcast(I32),
+                in_=x_scales[:, 1].bitcast(I32),
+            )
+
+        def unpad_x_scales(c):
+            nc.vector.tensor_copy(
+                out=x_scales[:, c + 1].bitcast(I32),
+                in_=x_scales_padded[:, c + 1, :, ROW : ROW + COLS].bitcast(I32),
             )
 
         w1_raw = {}
@@ -115,79 +138,100 @@ def tile_parallelnca_pa_kernel(tc, x, w1, b1, w2, b2, out):
         w1_codes = {}
         w1_scales = {}
 
-        def load_unit(k):
+        def load_unit(k, pieces=1):
             m, t = divmod(k, TILES)
             u, e = divmod(t, 2)
+            for i in w2_tiles(k):
+                if i % TILES == 0:
+                    n = i // TILES
+                    w2_raw[n] = pair_pool.tile([P, TILES, STRETCH], BF16, name="w2_raw", tag="w2_raw")
+                    nc.sync.dma_start(
+                        out=w2_raw[n][:].rearrange("p (u e) k -> p u (e k)", u=2), in_=w2_rows[n]
+                    )
             w1_raw[k] = raw_pool.tile([P, NS * STRETCH], BF16, name="w1_raw", tag="w1_raw")
-            nc.sync.dma_start(out=w1_raw[k][:], in_=w1_rows[m, u, e])
-            if t == 0:
-                w2_raw[m] = pair_pool.tile([P, TILES, STRETCH], BF16, name="w2_raw", tag="w2_raw")
-                nc.sync.dma_start(
-                    out=w2_raw[m][:].rearrange("p (u e) k -> p u (e k)", u=2), in_=w2_rows[m]
-                )
+            width = NS * STRETCH // pieces
+            for lo in range(0, NS * STRETCH, width):
+                nc.sync.dma_start(out=w1_raw[k][:, lo : lo + width], in_=w1_rows[m, u, e, :, lo : lo + width])
 
         def transpose_unit(k):
-            m, t = divmod(k, TILES)
             words = w1_raw[k][:].bitcast(F32)
             blocks = [words[:, WORDS * j : WORDS * (j + 1)] for j in range(NS)]
-            blocks.append(w2_raw[m][:, t, :].bitcast(F32))
+            for i in w2_tiles(k):
+                blocks.append(w2_raw[i // TILES][:, i % TILES, :].bitcast(F32))
             w_grouped[k] = pair_pool.tile(
-                [P, BLOCKS * STRETCH], BF16, name="w_grouped", tag="w_grouped", align_bytes=64
+                [P, MAX_BLOCKS * STRETCH], BF16, name="w_grouped", tag="w_grouped", align_bytes=64
             )
             grouped_words = w_grouped[k][:].bitcast(F32).rearrange("p (b r u) -> p b r u", r=P, u=2)
-            for first in range(0, BLOCKS, 2):
+            for first in range(0, len(blocks), 2):
+                count = min(2, len(blocks) - first)
                 bank = turn_psum.tile([P, 2, 2, P], F32, tag="turned")
-                for a in range(2):
+                for a in range(count):
                     for u in range(2):
                         nc.tensor.transpose(
                             bank[:, a, u, :], blocks[first + a][:, P * u : P * (u + 1)], identity[:]
                         )
                 nc.scalar.copy(
-                    out=grouped_words[:, first : first + 2],
-                    in_=bank[:].rearrange("p a u r -> p a r u"),
+                    out=grouped_words[:, first : first + count],
+                    in_=bank[:, 0:count].rearrange("p a u r -> p a r u"),
                 )
 
-        def quantise_unit(k):
-            m, t = divmod(k, TILES)
-            w1_codes[k] = code_pool.tile([P, NS * P], U32, name="w1_codes", tag="w1_codes", align_bytes=64)
-            w1_scales[k] = code_pool.tile([P, NS * P], U8, name="w1_scales", tag="w1_scales", align_bytes=64)
-            for lo, hi in ((0, NS - 1), (NS - 1, NS)):
-                nc.vector.quantize_mx(
-                    out=w1_codes[k][:, P * lo : P * hi].bitcast(FP8X4),
-                    scales=w1_scales[k][:, P * lo : P * hi],
-                    in_=w_grouped[k][:, STRETCH * lo : STRETCH * hi],
-                )
+        def quantise_w1(k, lo, hi):
+            if k not in w1_codes:
+                w1_codes[k] = code_pool.tile([P, NS * P], U32, name="w1_codes", tag="w1_codes", align_bytes=64)
+                w1_scales[k] = code_pool.tile([P, NS * P], U8, name="w1_scales", tag="w1_scales", align_bytes=64)
             nc.vector.quantize_mx(
-                out=w2_codes[:, m, P * t : P * (t + 1)].bitcast(FP8X4),
-                scales=w2_scales[:, m, P * t : P * (t + 1)],
-                in_=w_grouped[k][:, STRETCH * NS : STRETCH * BLOCKS],
+                out=w1_codes[k][:, P * lo : P * hi].bitcast(FP8X4),
+                scales=w1_scales[k][:, P * lo : P * hi],
+                in_=w_grouped[k][:, STRETCH * lo : STRETCH * hi],
             )
 
+        def quantise_unit(k):
+            quantise_w1(k, 0, NS - 1)
+            quantise_w1(k, NS - 1, NS)
+            tiles = w2_tiles(k)
+            if tiles:
+                m, t = divmod(tiles[0], TILES)
+                columns = slice(P * t, P * (t + len(tiles)))
+                nc.vector.quantize_mx(
+                    out=w2_codes[:, m, columns].bitcast(FP8X4),
+                    scales=w2_scales[:, m, columns],
+                    in_=w_grouped[k][:, STRETCH * NS : STRETCH * (NS + len(tiles))],
+                )
+
+        accs = {}
         hidden = {}
         hidden_codes = {}
         hidden_scales = {}
         out_tiles = {}
 
-        def first_product(k):
-            m, t = divmod(k, TILES)
-            acc = acc_psum.tile([P, COLS], F32, tag="acc")
-            for j in range(NS):
-                copy_number, g = divmod(m * NS + j, GROUPS)
-                r, c = SHIFTS[copy_number]
+        def shift_of(m, j):
+            copy_number, g = divmod(m * NS + j, GROUPS)
+            return SHIFTS[copy_number] + (g,)
+
+        def first_passes(k, passes, start, stop):
+            m = k // TILES
+            if start:
+                accs[k] = acc_psum.tile([P, COLS], F32, name="acc", tag="acc")
+            for j in passes:
+                r, c, g = shift_of(m, j)
                 window = slice(ROW * (1 + r), ROW * (1 + r) + COLS)
                 if r == 0:
                     rhs_scale = x_scales[:, c + 1, g, :]
                 else:
                     rhs_scale = x_scales_padded[:, c + 1, g, window]
                 nc.tensor.matmul_mx(
-                    out=acc[:],
+                    out=accs[k][:],
                     lhsT=w1_codes[k][:, P * j : P * (j + 1)].bitcast(FP8X4),
                     lhsT_scale=w1_scales[k][:, P * j : P * (j + 1)],
                     rhs=x_codes[:, c + 1, g, window].bitcast(FP8X4),
                     rhs_scale=rhs_scale,
-                    start=(j == 0),
-                    stop=(j == NS - 1),
+                    start=start and j == passes[0],
+                    stop=stop and j == passes[-1],
                 )
+
+        def activate(k):
+            m, t = divmod(k, TILES)
+            acc = accs[k]
             if t == 0:
                 hidden[m] = pair_pool.tile([P, TILES, COLS], BF16, name="hidden", tag="hidden")
             nc.scalar.activation(
@@ -197,6 +241,10 @@ def tile_parallelnca_pa_kernel(tc, x, w1, b1, w2, b2, out):
                 bias=bias[:, k : k + 1],
                 scale=1.0,
             )
+
+        def first_product(k):
+            first_passes(k, range(NS), True, True)
+            activate(k)
 
         def quantise_hidden(m):
             grouped = pair_pool.tile([P, COLS, PACK], BF16, tag="hidden_grouped", align_bytes=64)
@@ -241,52 +289,65 @@ def tile_parallelnca_pa_kernel(tc, x, w1, b1, w2, b2, out):
 
         for g in range(GROUPS):
             load_x(g)
-        load_unit(0)
+        load_unit(0, pieces=3)
         nc.sync.dma_start(out=bias_rows[0:8, :], in_=b1.rearrange("(r c) -> r c", c=2 * P))
         nc.sync.dma_start(out=bias_rows[8:16, :], in_=b2.rearrange("(r c) -> r c", c=2 * P))
-        for k in range(1, RAW_BUFS):
+        load_unit(1, pieces=3)
+        for k in range(2, RAW_BUFS):
             load_unit(k)
 
-        left = {}
         for g in range(GROUPS + 1):
             if g < GROUPS:
                 regroup_x(g)
             if g > 0:
-                quantise_x(0, g - 1, x_centre[:, g - 1])
-                left[g - 1] = shift_x(-1, g - 1)
-        pad_x_scales(0)
+                quantise_x(g - 1)
 
+        unshifted = [j for j in range(NS) if shift_of(0, j)[1] == 0]
+        shifted = [j for j in range(NS) if shift_of(0, j)[1] != 0]
         transpose_unit(0)
         load_unit(RAW_BUFS)
+        quantise_w1(0, 0, 4)
+        pad_x_scales()
+        quantise_w1(0, NS - 1, NS)
+        shift_words(-1, 0, GROUPS)
+        quantise_w1(0, 4, NS - 1)
+        shift_scales(-1)
+        first_passes(0, unshifted, True, False)
+        transpose_unit(1)
+        load_unit(RAW_BUFS + 1)
         bias_bank = turn_psum.tile([P, 2, 2, P], F32, tag="turned")
         nc.tensor.transpose(bias_bank[:, 0, 0, :], bias_rows[:].bitcast(F32), identity[:])
         nc.vector.tensor_copy(out=bias[:], in_=bias_bank[:, 0, 0, 0:UNITS].bitcast(BF16))
-        quantise_unit(0)
-        for g in range(GROUPS):
-            quantise_x(-1, g, left[g])
-        pad_x_scales(-1)
-        transpose_unit(1)
-        load_unit(RAW_BUFS + 1)
+        first_passes(0, shifted, False, True)
+        activate(0)
         quantise_unit(1)
+        transpose_unit(2)
+        load_unit(RAW_BUFS + 2)
+        quantise_unit(2)
+        shift_words(1, 0, 2)
+        shift_scales(1)
+        first_product(1)
+        transpose_unit(3)
+        load_unit(RAW_BUFS + 3)
+        quantise_unit(3)
+        shift_words(1, 2, GROUPS)
+        unpad_x_scales(-1)
+        unpad_x_scales(1)
 
-        for k in range(UNITS):
+        for k in range(2, UNITS):
             m, t = divmod(k, TILES)
+            first_passes(k, range(BEFORE), True, False)
             if k + AHEAD < UNITS:
                 transpose_unit(k + AHEAD)
             if k + AHEAD + RAW_BUFS < UNITS:
                 load_unit(k + AHEAD + RAW_BUFS)
-            if m == 0:
-                right = shift_x(1, t)
             if k + AHEAD < UNITS:
                 quantise_unit(k + AHEAD)
-            if m == 0:
-                quantise_x(1, t, right)
-            first_product(k)
+            first_passes(k, range(BEFORE, NS), False, True)
+            activate(k)
             if m > 0:
                 second_product(m - 1, t)
             if t == TILES - 1:
                 quantise_hidden(m)
-                if m == 0:
-                    pad_x_scales(1)
         for t in range(TILES):
             second_product(GROUPS - 1, t)

@@ -30,6 +30,7 @@ BANKS = 5
 FIRST_W2 = 3
 AHEAD = 2
 BEFORE = NS // 2
+WARM = 48
 RAW_BUFS = 4
 
 
@@ -61,6 +62,7 @@ def tile_parallelnca_pa_kernel(tc, x, w1, b1, w2, b2, out):
         ctx.enter_context(tc.manual_schedule())
 
         identity = keep.tile([P, P], F32, name="identity")
+        idle = keep.tile([P, P], BF16, name="idle")
         bias_rows = keep.tile([P, 2 * P], BF16, name="bias_rows")
         bias = keep.tile([P, 2 * UNITS], F32, name="bias")
         x_raw = keep.tile([P, BATCH, GROUPS, PACK, PIXELS], BF16, name="x_raw")
@@ -75,10 +77,12 @@ def tile_parallelnca_pa_kernel(tc, x, w1, b1, w2, b2, out):
             words = x_codes[:, c + 1, lo:hi, ROW : ROW + COLS].bitcast(I32)
             return words.rearrange("q g (a j) -> q g a j", j=GRID)
 
+        nc.gpsimd.memset(idle[:], 0.0)
+        nc.gpsimd.memset(x_scales[:, 1].bitcast(I32), 0)
+        nc.gpsimd.memset(bias_rows[:], 0.0)
         make_identity(nc, identity[:])
-        nc.vector.memset(bias_rows[:], 0.0)
-        nc.vector.memset(x_scales[:, 1].bitcast(I32), 0)
-        nc.vector.memset(x_scales_padded[:].bitcast(I32), 0)
+        nc.vector.memset(x_scales_padded[:, :, :, 0 : ROW + 4].bitcast(I32), 0)
+        nc.vector.memset(x_scales_padded[:, :, :, ROW + COLS - 4 : PADDED].bitcast(I32), 0)
         nc.vector.memset(x_codes[:, :, :, 0:ROW].bitcast(I32), 0)
         nc.vector.memset(x_codes[:, :, :, ROW + COLS : PADDED].bitcast(I32), 0)
         for c in (-1, 1):
@@ -96,8 +100,8 @@ def tile_parallelnca_pa_kernel(tc, x, w1, b1, w2, b2, out):
             grouped = x_centre[:, g].rearrange("q (i n) j t -> q i n j t", n=BATCH)
             for n, copy in ((0, nc.vector.tensor_copy), (1, nc.scalar.copy)):
                 copy(
-                    out=grouped[:, :, n],
-                    in_=x_raw[:, n, g].rearrange("q t (i j) -> q i j t", j=GRID),
+                    out=grouped[:, :, n].rearrange("q i (c s) t -> q i c t s", s=4),
+                    in_=x_raw[:, n, g].rearrange("q t (i c s) -> q i c t s", c=GRID // 4, s=4),
                 )
 
         def quantise_x(g):
@@ -208,19 +212,28 @@ def tile_parallelnca_pa_kernel(tc, x, w1, b1, w2, b2, out):
             copy_number, g = divmod(m * NS + j, GROUPS)
             return SHIFTS[copy_number] + (g,)
 
-        def first_passes(k, passes, start, stop):
+        def pieces_of(m):
+            half = COLS // 2
+            return [(0, half), (half, COLS)] if m == GROUPS - 1 else [(0, COLS)]
+
+        def new_bank(at_end):
+            if at_end:
+                return turn_psum.tile([P, COLS], F32, name="acc", tag="turned")
+            return acc_psum.tile([P, COLS], F32, name="acc", tag="acc")
+
+        def first_passes(k, passes, start, stop, lo=0, hi=COLS):
             m = k // TILES
             if start:
-                accs[k] = acc_psum.tile([P, COLS], F32, name="acc", tag="acc")
+                accs[k, lo] = new_bank(k == UNITS - 1)
             for j in passes:
                 r, c, g = shift_of(m, j)
-                window = slice(ROW * (1 + r), ROW * (1 + r) + COLS)
+                window = slice(ROW * (1 + r) + lo, ROW * (1 + r) + hi)
                 if r == 0:
-                    rhs_scale = x_scales[:, c + 1, g, :]
+                    rhs_scale = x_scales[:, c + 1, g, lo:hi]
                 else:
                     rhs_scale = x_scales_padded[:, c + 1, g, window]
                 nc.tensor.matmul_mx(
-                    out=accs[k][:],
+                    out=accs[k, lo][:, 0 : hi - lo],
                     lhsT=w1_codes[k][:, P * j : P * (j + 1)].bitcast(FP8X4),
                     lhsT_scale=w1_scales[k][:, P * j : P * (j + 1)],
                     rhs=x_codes[:, c + 1, g, window].bitcast(FP8X4),
@@ -229,63 +242,69 @@ def tile_parallelnca_pa_kernel(tc, x, w1, b1, w2, b2, out):
                     stop=stop and j == passes[-1],
                 )
 
-        def activate(k):
+        def activate(k, lo=0, hi=COLS, base=0):
             m, t = divmod(k, TILES)
-            acc = accs[k]
-            if t == 0:
-                hidden[m] = pair_pool.tile([P, TILES, COLS], BF16, name="hidden", tag="hidden")
+            if (m, lo) not in hidden:
+                hidden[m, lo] = pair_pool.tile([P, TILES, COLS], BF16, name="hidden", tag="hidden")
             nc.scalar.activation(
-                out=hidden[m][:, t, :].rearrange("p (n i j) -> p n i j", n=BATCH, j=GRID),
-                in_=acc[:].rearrange("p (i n j) -> p n i j", n=BATCH, j=GRID),
+                out=hidden[m, lo][:, t, 0 : hi - lo].rearrange("p (n i j) -> p n i j", n=BATCH, j=GRID),
+                in_=accs[k, base][:, lo - base : hi - base].rearrange("p (i n j) -> p n i j", n=BATCH, j=GRID),
                 func=RELU,
                 bias=bias[:, k : k + 1],
                 scale=1.0,
             )
 
-        def first_product(k):
-            first_passes(k, range(NS), True, True)
-            activate(k)
-
-        def quantise_hidden(m):
+        def quantise_hidden(m, lo=0, hi=COLS):
+            width = hi - lo
             grouped = pair_pool.tile([P, COLS, PACK], BF16, tag="hidden_grouped", align_bytes=64)
             nc.vector.tensor_copy(
-                out=grouped[:].rearrange("p (c i) t -> p c t i", i=4),
-                in_=hidden[m][:].rearrange("p t (c i) -> p c t i", i=4),
+                out=grouped[:, 0:width].rearrange("p (c i) t -> p c t i", i=4),
+                in_=hidden[m, lo][:, :, 0:width].rearrange("p t (c i) -> p c t i", i=4),
             )
-            hidden_codes[m] = pair_pool.tile([P, COLS], U32, name="hidden_codes", tag="hidden_codes", align_bytes=64)
-            hidden_scales[m] = pair_pool.tile([P, COLS], U8, name="hidden_scales", tag="hidden_scales", align_bytes=64)
+            codes = pair_pool.tile([P, COLS], U32, name="hidden_codes", tag="hidden_codes", align_bytes=64)
+            scales = pair_pool.tile([P, COLS], U8, name="hidden_scales", tag="hidden_scales", align_bytes=64)
+            hidden_codes[m, lo], hidden_scales[m, lo] = codes, scales
             nc.vector.quantize_mx(
-                out=hidden_codes[m][:].bitcast(FP8X4),
-                scales=hidden_scales[m][:],
-                in_=grouped[:].rearrange("p w t -> p (w t)"),
+                out=codes[:, 0:width].bitcast(FP8X4),
+                scales=scales[:, 0:width],
+                in_=grouped[:, 0:width].rearrange("p w t -> p (w t)"),
             )
 
-        def second_product(m, t):
-            u, e = divmod(t, 2)
-            acc = acc_psum.tile([P, COLS], F32, tag="acc")
+        def second_product(m, t, lo=0, hi=COLS):
+            accs[m, t, lo] = new_bank(m == GROUPS - 1)
             nc.tensor.matmul_mx(
-                out=acc[:],
+                out=accs[m, t, lo][:, 0 : hi - lo],
                 lhsT=w2_codes[:, m, P * t : P * (t + 1)].bitcast(FP8X4),
                 lhsT_scale=w2_scales[:, m, P * t : P * (t + 1)],
-                rhs=hidden_codes[m][:].bitcast(FP8X4),
-                rhs_scale=hidden_scales[m][:],
+                rhs=hidden_codes[m, lo][:, 0 : hi - lo].bitcast(FP8X4),
+                rhs_scale=hidden_scales[m, lo][:, 0 : hi - lo],
                 start=True,
                 stop=True,
             )
-            if e == 0:
+
+        def finish(m, t, lo=0, hi=COLS):
+            u, e = divmod(t, 2)
+            pixels = slice(lo // BATCH, hi // BATCH)
+            if (m, u) not in out_tiles:
                 out_tiles[m, u] = out_pool.tile([P, BATCH, 2, PIXELS], F32, name="out_tile", tag="out_tile")
             nc.vector.scalar_tensor_tensor(
-                out=out_tiles[m, u][:, :, e, :],
-                in0=acc[:].rearrange("p (n f) -> p n f", n=BATCH),
+                out=out_tiles[m, u][:, :, e, pixels],
+                in0=accs[m, t, lo][:, 0 : hi - lo].rearrange("p (n f) -> p n f", n=BATCH),
                 scalar=bias[:, UNITS + TILES * m + t : UNITS + TILES * m + t + 1],
-                in1=x_raw[:, :, m, t, :],
+                in1=x_raw[:, :, m, t, pixels],
                 op0=ADD,
                 op1=ADD,
             )
-            if e == 1:
+            if e == 1 and hi - lo == COLS:
                 nc.sync.dma_start(
                     out=out_rows[m, u], in_=out_tiles[m, u][:].rearrange("p n e f -> p n (e f)")
                 )
+            elif e == 1:
+                for n in range(BATCH):
+                    nc.sync.dma_start(
+                        out=out_rows[m, u, :, n].rearrange("p (e f) -> p e f", e=2)[:, :, pixels],
+                        in_=out_tiles[m, u][:, n, :, pixels],
+                    )
 
         for g in range(GROUPS):
             load_x(g)
@@ -295,6 +314,10 @@ def tile_parallelnca_pa_kernel(tc, x, w1, b1, w2, b2, out):
         load_unit(1, pieces=3)
         for k in range(2, RAW_BUFS):
             load_unit(k)
+
+        idle_bank = turn_psum.tile([P, COLS], F32, name="idle_bank", tag="turned")
+        for i in range(WARM):
+            nc.tensor.matmul(idle_bank[:, 0:P], idle[:], idle[:], start=True, stop=True)
 
         for g in range(GROUPS + 1):
             if g < GROUPS:
@@ -306,12 +329,12 @@ def tile_parallelnca_pa_kernel(tc, x, w1, b1, w2, b2, out):
         shifted = [j for j in range(NS) if shift_of(0, j)[1] != 0]
         transpose_unit(0)
         load_unit(RAW_BUFS)
+        shift_words(-1, 0, GROUPS)
         quantise_w1(0, 0, 4)
         pad_x_scales()
         quantise_w1(0, NS - 1, NS)
-        shift_words(-1, 0, GROUPS)
-        quantise_w1(0, 4, NS - 1)
         shift_scales(-1)
+        quantise_w1(0, 4, NS - 1)
         first_passes(0, unshifted, True, False)
         transpose_unit(1)
         load_unit(RAW_BUFS + 1)
@@ -326,7 +349,8 @@ def tile_parallelnca_pa_kernel(tc, x, w1, b1, w2, b2, out):
         quantise_unit(2)
         shift_words(1, 0, 2)
         shift_scales(1)
-        first_product(1)
+        first_passes(1, range(NS), True, True)
+        activate(1)
         transpose_unit(3)
         load_unit(RAW_BUFS + 3)
         quantise_unit(3)
@@ -334,7 +358,7 @@ def tile_parallelnca_pa_kernel(tc, x, w1, b1, w2, b2, out):
         unpad_x_scales(-1)
         unpad_x_scales(1)
 
-        for k in range(2, UNITS):
+        for k in range(2, UNITS - 1):
             m, t = divmod(k, TILES)
             first_passes(k, range(BEFORE), True, False)
             if k + AHEAD < UNITS:
@@ -344,10 +368,30 @@ def tile_parallelnca_pa_kernel(tc, x, w1, b1, w2, b2, out):
             if k + AHEAD < UNITS:
                 quantise_unit(k + AHEAD)
             first_passes(k, range(BEFORE, NS), False, True)
-            activate(k)
+            for lo, hi in pieces_of(m):
+                activate(k, lo, hi)
             if m > 0:
                 second_product(m - 1, t)
+                finish(m - 1, t)
             if t == TILES - 1:
                 quantise_hidden(m)
+
+        last = GROUPS - 1
+        second_product(last - 1, TILES - 1)
+        finish(last - 1, TILES - 1)
+        (lo, mid), (mid, hi) = pieces_of(last)
+        first_passes(UNITS - 1, range(NS), True, True, lo, mid)
+        activate(UNITS - 1, lo, mid, lo)
+        quantise_hidden(last, lo, mid)
+        first_passes(UNITS - 1, range(NS), True, True, mid, hi)
+        activate(UNITS - 1, mid, hi, mid)
         for t in range(TILES):
-            second_product(GROUPS - 1, t)
+            second_product(last, t, lo, mid)
+        finish(last, 0, lo, mid)
+        finish(last, 1, lo, mid)
+        quantise_hidden(last, mid, hi)
+        finish(last, 2, lo, mid)
+        finish(last, 3, lo, mid)
+        for t in range(TILES):
+            second_product(last, t, mid, hi)
+            finish(last, t, mid, hi)

@@ -18,6 +18,7 @@ STRETCH = P * PACK
 WORDS = STRETCH // 2
 
 BATCH, GROUPS, GRID = 2, 4, 16
+LIVE = 4
 PIXELS = GRID * GRID
 COLS = BATCH * PIXELS
 ROW = BATCH * GRID
@@ -30,7 +31,6 @@ BANKS = 5
 FIRST_W2 = 3
 AHEAD = 2
 BEFORE = NS // 2
-WARM = 48
 RAW_BUFS = 4
 
 
@@ -56,7 +56,7 @@ def tile_parallelnca_pa_kernel(tc, x, w1, b1, w2, b2, out):
         raw_pool = ctx.enter_context(tc.tile_pool(name="raw_pool", bufs=RAW_BUFS))
         pair_pool = ctx.enter_context(tc.tile_pool(name="pair_pool", bufs=2))
         code_pool = ctx.enter_context(tc.tile_pool(name="code_pool", bufs=AHEAD + 1))
-        out_pool = ctx.enter_context(tc.tile_pool(name="out_pool", bufs=3))
+        out_pool = ctx.enter_context(tc.tile_pool(name="out_pool", bufs=4))
         turn_psum = ctx.enter_context(tc.psum_pool(name="turn_psum", bufs=BANKS))
         acc_psum = ctx.enter_context(tc.psum_pool(name="acc_psum", bufs=3))
         ctx.enter_context(tc.manual_schedule())
@@ -68,8 +68,8 @@ def tile_parallelnca_pa_kernel(tc, x, w1, b1, w2, b2, out):
         x_raw = keep.tile([P, BATCH, GROUPS, PACK, PIXELS], BF16, name="x_raw")
         x_centre = keep.tile([P, GROUPS, GRID * BATCH, GRID, PACK], BF16, name="x_centre", align_bytes=64)
         x_codes = keep.tile([P, 3, GROUPS, PADDED], U32, name="x_codes", align_bytes=64)
-        x_scales = keep.tile([P, 3, GROUPS, COLS], U8, name="x_scales", align_bytes=64)
-        x_scales_padded = keep.tile([P, 3, GROUPS, PADDED], U8, name="x_scales_padded", align_bytes=64)
+        x_scales = keep.tile([P, 3, COLS], U8, name="x_scales", align_bytes=64)
+        x_scales_padded = keep.tile([P, 3, PADDED], U8, name="x_scales_padded", align_bytes=64)
         w2_codes = keep.tile([P, GROUPS, STRETCH], U32, name="w2_codes", align_bytes=64)
         w2_scales = keep.tile([P, GROUPS, STRETCH], U8, name="w2_scales", align_bytes=64)
 
@@ -81,8 +81,8 @@ def tile_parallelnca_pa_kernel(tc, x, w1, b1, w2, b2, out):
         nc.gpsimd.memset(x_scales[:, 1].bitcast(I32), 0)
         nc.gpsimd.memset(bias_rows[:], 0.0)
         make_identity(nc, identity[:])
-        nc.vector.memset(x_scales_padded[:, :, :, 0 : ROW + 4].bitcast(I32), 0)
-        nc.vector.memset(x_scales_padded[:, :, :, ROW + COLS - 4 : PADDED].bitcast(I32), 0)
+        nc.vector.memset(x_scales_padded[:, :, 0 : ROW + 4].bitcast(I32), 0)
+        nc.vector.memset(x_scales_padded[:, :, ROW + COLS - 4 : PADDED].bitcast(I32), 0)
         nc.vector.memset(x_codes[:, :, :, 0:ROW].bitcast(I32), 0)
         nc.vector.memset(x_codes[:, :, :, ROW + COLS : PADDED].bitcast(I32), 0)
         for c in (-1, 1):
@@ -107,7 +107,7 @@ def tile_parallelnca_pa_kernel(tc, x, w1, b1, w2, b2, out):
         def quantise_x(g):
             nc.vector.quantize_mx(
                 out=x_codes[:, 1, g, ROW : ROW + COLS].bitcast(FP8X4),
-                scales=x_scales[:, 1, g, :],
+                scales=x_scales[LIVE * g : P, 1, :],
                 in_=x_centre[:, g].rearrange("q a j t -> q (a j t)"),
             )
 
@@ -120,20 +120,20 @@ def tile_parallelnca_pa_kernel(tc, x, w1, b1, w2, b2, out):
 
         def shift_scales(c):
             nc.vector.tensor_copy(
-                out=x_scales_padded[:, c + 1, :, ROW - c : ROW - c + COLS],
+                out=x_scales_padded[:, c + 1, ROW - c : ROW - c + COLS],
                 in_=x_scales[:, 1],
             )
 
         def pad_x_scales():
             nc.vector.tensor_copy(
-                out=x_scales_padded[:, 1, :, ROW : ROW + COLS].bitcast(I32),
+                out=x_scales_padded[:, 1, ROW : ROW + COLS].bitcast(I32),
                 in_=x_scales[:, 1].bitcast(I32),
             )
 
         def unpad_x_scales(c):
             nc.vector.tensor_copy(
                 out=x_scales[:, c + 1].bitcast(I32),
-                in_=x_scales_padded[:, c + 1, :, ROW : ROW + COLS].bitcast(I32),
+                in_=x_scales_padded[:, c + 1, ROW : ROW + COLS].bitcast(I32),
             )
 
         w1_raw = {}
@@ -213,8 +213,10 @@ def tile_parallelnca_pa_kernel(tc, x, w1, b1, w2, b2, out):
             return SHIFTS[copy_number] + (g,)
 
         def pieces_of(m):
-            half = COLS // 2
-            return [(0, half), (half, COLS)] if m == GROUPS - 1 else [(0, COLS)]
+            half, quarter = COLS // 2, COLS // 4
+            if m == GROUPS - 1:
+                return [(0, half), (half, COLS - quarter), (COLS - quarter, COLS)]
+            return [(0, COLS)]
 
         def new_bank(at_end):
             if at_end:
@@ -224,14 +226,14 @@ def tile_parallelnca_pa_kernel(tc, x, w1, b1, w2, b2, out):
         def first_passes(k, passes, start, stop, lo=0, hi=COLS):
             m = k // TILES
             if start:
-                accs[k, lo] = new_bank(k == UNITS - 1)
+                accs[k, lo] = new_bank(k >= UNITS - 2)
             for j in passes:
                 r, c, g = shift_of(m, j)
                 window = slice(ROW * (1 + r) + lo, ROW * (1 + r) + hi)
                 if r == 0:
-                    rhs_scale = x_scales[:, c + 1, g, lo:hi]
+                    rhs_scale = x_scales[LIVE * g : P, c + 1, lo:hi]
                 else:
-                    rhs_scale = x_scales_padded[:, c + 1, g, window]
+                    rhs_scale = x_scales_padded[LIVE * g : P, c + 1, window]
                 nc.tensor.matmul_mx(
                     out=accs[k, lo][:, 0 : hi - lo],
                     lhsT=w1_codes[k][:, P * j : P * (j + 1)].bitcast(FP8X4),
@@ -242,12 +244,15 @@ def tile_parallelnca_pa_kernel(tc, x, w1, b1, w2, b2, out):
                     stop=stop and j == passes[-1],
                 )
 
+        def hidden_piece(m, lo, hi):
+            return hidden[m][:, TILES * lo : TILES * hi].rearrange("p (t f) -> p t f", t=TILES)
+
         def activate(k, lo=0, hi=COLS, base=0):
             m, t = divmod(k, TILES)
-            if (m, lo) not in hidden:
-                hidden[m, lo] = pair_pool.tile([P, TILES, COLS], BF16, name="hidden", tag="hidden")
+            if m not in hidden:
+                hidden[m] = pair_pool.tile([P, TILES * COLS], BF16, name="hidden", tag="hidden")
             nc.scalar.activation(
-                out=hidden[m, lo][:, t, 0 : hi - lo].rearrange("p (n i j) -> p n i j", n=BATCH, j=GRID),
+                out=hidden_piece(m, lo, hi)[:, t].rearrange("p (n i j) -> p n i j", n=BATCH, j=GRID),
                 in_=accs[k, base][:, lo - base : hi - base].rearrange("p (i n j) -> p n i j", n=BATCH, j=GRID),
                 func=RELU,
                 bias=bias[:, k : k + 1],
@@ -259,7 +264,7 @@ def tile_parallelnca_pa_kernel(tc, x, w1, b1, w2, b2, out):
             grouped = pair_pool.tile([P, COLS, PACK], BF16, tag="hidden_grouped", align_bytes=64)
             nc.vector.tensor_copy(
                 out=grouped[:, 0:width].rearrange("p (c i) t -> p c t i", i=4),
-                in_=hidden[m, lo][:, :, 0:width].rearrange("p t (c i) -> p c t i", i=4),
+                in_=hidden_piece(m, lo, hi).rearrange("p t (c i) -> p c t i", i=4),
             )
             codes = pair_pool.tile([P, COLS], U32, name="hidden_codes", tag="hidden_codes", align_bytes=64)
             scales = pair_pool.tile([P, COLS], U8, name="hidden_scales", tag="hidden_scales", align_bytes=64)
@@ -285,26 +290,30 @@ def tile_parallelnca_pa_kernel(tc, x, w1, b1, w2, b2, out):
         def finish(m, t, lo=0, hi=COLS):
             u, e = divmod(t, 2)
             pixels = slice(lo // BATCH, hi // BATCH)
-            if (m, u) not in out_tiles:
-                out_tiles[m, u] = out_pool.tile([P, BATCH, 2, PIXELS], F32, name="out_tile", tag="out_tile")
+            span = PIXELS if m < GROUPS - 1 else PIXELS // 2
+            first = pixels.start - pixels.start % span
+            if (m, u, first) not in out_tiles:
+                out_tiles[m, u, first] = out_pool.tile(
+                    [P, BATCH, 2, span], F32, name="out_tile", tag="out_tile"
+                )
+            out_tile = out_tiles[m, u, first]
             nc.vector.scalar_tensor_tensor(
-                out=out_tiles[m, u][:, :, e, pixels],
+                out=out_tile[:, :, e, pixels.start - first : pixels.stop - first],
                 in0=accs[m, t, lo][:, 0 : hi - lo].rearrange("p (n f) -> p n f", n=BATCH),
                 scalar=bias[:, UNITS + TILES * m + t : UNITS + TILES * m + t + 1],
                 in1=x_raw[:, :, m, t, pixels],
                 op0=ADD,
                 op1=ADD,
             )
-            if e == 1 and hi - lo == COLS:
-                nc.sync.dma_start(
-                    out=out_rows[m, u], in_=out_tiles[m, u][:].rearrange("p n e f -> p n (e f)")
-                )
-            elif e == 1:
-                for n in range(BATCH):
-                    nc.sync.dma_start(
-                        out=out_rows[m, u, :, n].rearrange("p (e f) -> p e f", e=2)[:, :, pixels],
-                        in_=out_tiles[m, u][:, n, :, pixels],
-                    )
+            if e == 1 and pixels.stop == first + span:
+                if span == PIXELS:
+                    nc.sync.dma_start(out=out_rows[m, u], in_=out_tile[:].rearrange("p n e f -> p n (e f)"))
+                else:
+                    for n in range(BATCH):
+                        nc.sync.dma_start(
+                            out=out_rows[m, u, :, n].rearrange("p (e f) -> p e f", e=2)[:, :, first : first + span],
+                            in_=out_tile[:, n],
+                        )
 
         for g in range(GROUPS):
             load_x(g)
@@ -316,8 +325,15 @@ def tile_parallelnca_pa_kernel(tc, x, w1, b1, w2, b2, out):
             load_unit(k)
 
         idle_bank = turn_psum.tile([P, COLS], F32, name="idle_bank", tag="turned")
-        for i in range(WARM):
-            nc.tensor.matmul(idle_bank[:, 0:P], idle[:], idle[:], start=True, stop=True)
+        for g in range(GROUPS):
+            for n in range(BATCH):
+                nc.tensor.matmul(
+                    idle_bank[:],
+                    idle[:],
+                    x_raw[:, n, g, 0:2].rearrange("q e f -> q (e f)"),
+                    start=True,
+                    stop=True,
+                )
 
         for g in range(GROUPS + 1):
             if g < GROUPS:
@@ -358,7 +374,7 @@ def tile_parallelnca_pa_kernel(tc, x, w1, b1, w2, b2, out):
         unpad_x_scales(-1)
         unpad_x_scales(1)
 
-        for k in range(2, UNITS - 1):
+        for k in range(2, UNITS - 2):
             m, t = divmod(k, TILES)
             first_passes(k, range(BEFORE), True, False)
             if k + AHEAD < UNITS:
@@ -377,21 +393,31 @@ def tile_parallelnca_pa_kernel(tc, x, w1, b1, w2, b2, out):
                 quantise_hidden(m)
 
         last = GROUPS - 1
+        ends = (UNITS - 2, UNITS - 1)
+        long, middle, short = pieces_of(last)
+
+        def end_passes(k, lo, hi):
+            first_passes(k, range(NS), True, True, lo, hi)
+            activate(k, lo, hi, lo)
+
+        def end_products(lo, hi):
+            for t in range(TILES):
+                second_product(last, t, lo, hi)
+                finish(last, t, lo, hi)
+
+        second_product(last - 1, TILES - 2)
+        finish(last - 1, TILES - 2)
+        end_passes(ends[0], *long)
         second_product(last - 1, TILES - 1)
         finish(last - 1, TILES - 1)
-        (lo, mid), (mid, hi) = pieces_of(last)
-        first_passes(UNITS - 1, range(NS), True, True, lo, mid)
-        activate(UNITS - 1, lo, mid, lo)
-        quantise_hidden(last, lo, mid)
-        first_passes(UNITS - 1, range(NS), True, True, mid, hi)
-        activate(UNITS - 1, mid, hi, mid)
-        for t in range(TILES):
-            second_product(last, t, lo, mid)
-        finish(last, 0, lo, mid)
-        finish(last, 1, lo, mid)
-        quantise_hidden(last, mid, hi)
-        finish(last, 2, lo, mid)
-        finish(last, 3, lo, mid)
-        for t in range(TILES):
-            second_product(last, t, mid, hi)
-            finish(last, t, mid, hi)
+        end_passes(ends[1], *long)
+        quantise_hidden(last, *long)
+        for k in ends:
+            end_passes(k, *middle)
+        quantise_hidden(last, *middle)
+        end_passes(ends[0], *short)
+        end_products(*long)
+        end_passes(ends[1], *short)
+        quantise_hidden(last, *short)
+        end_products(*middle)
+        end_products(*short)

@@ -30,7 +30,6 @@ UNITS = GROUPS * TILES
 BANKS = 5
 FIRST_W2 = 3
 AHEAD = 2
-BEFORE = NS // 2
 RAW_BUFS = 4
 
 
@@ -55,7 +54,7 @@ def tile_parallelnca_pa_kernel(tc, x, w1, b1, w2, b2, out):
         keep = ctx.enter_context(tc.tile_pool(name="keep", bufs=1))
         raw_pool = ctx.enter_context(tc.tile_pool(name="raw_pool", bufs=RAW_BUFS))
         pair_pool = ctx.enter_context(tc.tile_pool(name="pair_pool", bufs=2))
-        code_pool = ctx.enter_context(tc.tile_pool(name="code_pool", bufs=AHEAD + 1))
+        code_pool = ctx.enter_context(tc.tile_pool(name="code_pool", bufs=AHEAD + 2))
         out_pool = ctx.enter_context(tc.tile_pool(name="out_pool", bufs=4))
         turn_psum = ctx.enter_context(tc.psum_pool(name="turn_psum", bufs=BANKS))
         acc_psum = ctx.enter_context(tc.psum_pool(name="acc_psum", bufs=3))
@@ -157,7 +156,7 @@ def tile_parallelnca_pa_kernel(tc, x, w1, b1, w2, b2, out):
             for lo in range(0, NS * STRETCH, width):
                 nc.sync.dma_start(out=w1_raw[k][:, lo : lo + width], in_=w1_rows[m, u, e, :, lo : lo + width])
 
-        def transpose_unit(k):
+        def transpose_unit(k, helped=False):
             words = w1_raw[k][:].bitcast(F32)
             blocks = [words[:, WORDS * j : WORDS * (j + 1)] for j in range(NS)]
             for i in w2_tiles(k):
@@ -174,7 +173,8 @@ def tile_parallelnca_pa_kernel(tc, x, w1, b1, w2, b2, out):
                         nc.tensor.transpose(
                             bank[:, a, u, :], blocks[first + a][:, P * u : P * (u + 1)], identity[:]
                         )
-                nc.scalar.copy(
+                copy = nc.vector.tensor_copy if helped and first // 2 % 2 else nc.scalar.copy
+                copy(
                     out=grouped_words[:, first : first + count],
                     in_=bank[:, 0:count].rearrange("p a u r -> p a r u"),
                 )
@@ -211,6 +211,11 @@ def tile_parallelnca_pa_kernel(tc, x, w1, b1, w2, b2, out):
         def shift_of(m, j):
             copy_number, g = divmod(m * NS + j, GROUPS)
             return SHIFTS[copy_number] + (g,)
+
+        def turned_in(k):
+            if k < TILES:
+                return [k + AHEAD]
+            return [i for i in (k + AHEAD, k + AHEAD + 1) if k % 2 == 0 and i < UNITS]
 
         def pieces_of(m):
             half, quarter = COLS // 2, COLS // 4
@@ -345,9 +350,9 @@ def tile_parallelnca_pa_kernel(tc, x, w1, b1, w2, b2, out):
         shifted = [j for j in range(NS) if shift_of(0, j)[1] != 0]
         transpose_unit(0)
         load_unit(RAW_BUFS)
-        shift_words(-1, 0, GROUPS)
-        quantise_w1(0, 0, 4)
         pad_x_scales()
+        quantise_w1(0, 0, 4)
+        shift_words(-1, 0, GROUPS)
         quantise_w1(0, NS - 1, NS)
         shift_scales(-1)
         quantise_w1(0, 4, NS - 1)
@@ -376,14 +381,16 @@ def tile_parallelnca_pa_kernel(tc, x, w1, b1, w2, b2, out):
 
         for k in range(2, UNITS - 2):
             m, t = divmod(k, TILES)
-            first_passes(k, range(BEFORE), True, False)
-            if k + AHEAD < UNITS:
-                transpose_unit(k + AHEAD)
-            if k + AHEAD + RAW_BUFS < UNITS:
-                load_unit(k + AHEAD + RAW_BUFS)
+            turned = turned_in(k)
+            before = NS - 1 if len(turned) == 2 else NS // 2
+            first_passes(k, range(before), True, False)
+            for i in turned:
+                transpose_unit(i, helped=i < turned[-1])
+                if i + RAW_BUFS < UNITS:
+                    load_unit(i + RAW_BUFS)
             if k + AHEAD < UNITS:
                 quantise_unit(k + AHEAD)
-            first_passes(k, range(BEFORE, NS), False, True)
+            first_passes(k, range(before, NS), False, True)
             for lo, hi in pieces_of(m):
                 activate(k, lo, hi)
             if m > 0:

@@ -89,8 +89,8 @@ def tile_parallelnca_pa_kernel(tc, x, w1, b1, w2, b2, out):
             nc.vector.memset(x_words(c, 0, GROUPS)[:, :, :, border], 0)
 
         def load_x(g):
-            for n in range(BATCH):
-                nc.sync.dma_start(
+            for n, queue in ((0, nc.sync), (1, nc.scalar)):
+                queue.dma_start(
                     out=x_raw[:, n, g].rearrange("q (u e) f -> q u (e f)", u=2),
                     in_=x_rows[g, n],
                 )

@@ -28,16 +28,11 @@ NS = len(SHIFTS)
 TILES = STRETCH // P
 UNITS = GROUPS * TILES
 BANKS = 5
-FIRST_W2 = 3
 AHEAD = 2
 RAW_BUFS = 4
-
-
-def w2_tiles(k):
-    return [i for i in range(UNITS) if max(FIRST_W2 + i // 2, i) == k]
-
-
-MAX_BLOCKS = NS + max(len(w2_tiles(k)) for k in range(UNITS))
+QUAD = 32
+QUADS = P // QUAD
+SETS = STRETCH // QUAD
 
 FLOPS = 2 * COLS * GROUPS * STRETCH * (NS * STRETCH + STRETCH)
 
@@ -47,7 +42,7 @@ def tile_parallelnca_pa_kernel(tc, x, w1, b1, w2, b2, out):
 
     x_rows = x.rearrange("n (g u q e) h w -> g n q u (e h w)", g=GROUPS, u=2, e=2)
     w1_rows = w1.rearrange("m (u p e) k -> m u e p k", u=2, e=2)
-    w2_rows = w2.rearrange("m (u p e) k -> m p u (e k)", u=2, e=2)
+    w2_runs = w2.rearrange("m (b f) (u q k) -> m q u f b k", f=QUAD, u=2, q=QUADS)
     out_rows = out.rearrange("n (m u p e) h w -> m u p n (e h w)", m=GROUPS, u=2, e=2)
 
     with ExitStack() as ctx:
@@ -137,6 +132,8 @@ def tile_parallelnca_pa_kernel(tc, x, w1, b1, w2, b2, out):
 
         w1_raw = {}
         w2_raw = {}
+        w2_turned = {}
+        w2_grouped = {}
         w_grouped = {}
         w1_codes = {}
         w1_scales = {}
@@ -144,13 +141,6 @@ def tile_parallelnca_pa_kernel(tc, x, w1, b1, w2, b2, out):
         def load_unit(k, pieces=1):
             m, t = divmod(k, TILES)
             u, e = divmod(t, 2)
-            for i in w2_tiles(k):
-                if i % TILES == 0:
-                    n = i // TILES
-                    w2_raw[n] = pair_pool.tile([P, TILES, STRETCH], BF16, name="w2_raw", tag="w2_raw")
-                    nc.sync.dma_start(
-                        out=w2_raw[n][:].rearrange("p (u e) k -> p u (e k)", u=2), in_=w2_rows[n]
-                    )
             w1_raw[k] = raw_pool.tile([P, NS * STRETCH], BF16, name="w1_raw", tag="w1_raw")
             width = NS * STRETCH // pieces
             for lo in range(0, NS * STRETCH, width):
@@ -159,10 +149,8 @@ def tile_parallelnca_pa_kernel(tc, x, w1, b1, w2, b2, out):
         def transpose_unit(k, helped=False):
             words = w1_raw[k][:].bitcast(F32)
             blocks = [words[:, WORDS * j : WORDS * (j + 1)] for j in range(NS)]
-            for i in w2_tiles(k):
-                blocks.append(w2_raw[i // TILES][:, i % TILES, :].bitcast(F32))
             w_grouped[k] = pair_pool.tile(
-                [P, MAX_BLOCKS * STRETCH], BF16, name="w_grouped", tag="w_grouped", align_bytes=64
+                [P, NS * STRETCH], BF16, name="w_grouped", tag="w_grouped", align_bytes=64
             )
             grouped_words = w_grouped[k][:].bitcast(F32).rearrange("p (b r u) -> p b r u", r=P, u=2)
             for first in range(0, len(blocks), 2):
@@ -192,15 +180,34 @@ def tile_parallelnca_pa_kernel(tc, x, w1, b1, w2, b2, out):
         def quantise_unit(k):
             quantise_w1(k, 0, NS - 1)
             quantise_w1(k, NS - 1, NS)
-            tiles = w2_tiles(k)
-            if tiles:
-                m, t = divmod(tiles[0], TILES)
-                columns = slice(P * t, P * (t + len(tiles)))
-                nc.vector.quantize_mx(
-                    out=w2_codes[:, m, columns].bitcast(FP8X4),
-                    scales=w2_scales[:, m, columns],
-                    in_=w_grouped[k][:, STRETCH * NS : STRETCH * (NS + len(tiles))],
-                )
+
+        def load_w2(m):
+            w2_raw[m] = pair_pool.tile([P, 2, SETS, 2 * QUAD], BF16, name="w2_raw", tag="w2_raw", align_bytes=64)
+            for q in range(QUADS):
+                for u in range(2):
+                    nc.sync.dma_start(
+                        out=w2_raw[m][QUAD * q : QUAD * (q + 1), u], in_=w2_runs[m, q, u]
+                    )
+
+        def turn_w2(m):
+            w2_turned[m] = pair_pool.tile([P, SETS * 2 * QUAD], F32, name="w2_turned", tag="w2_turned", align_bytes=64)
+            nc.vector.transpose(w2_turned[m][:], w2_raw[m][:].rearrange("p u b k -> p (u b k)").bitcast(F32))
+
+        def regroup_w2(m):
+            w2_grouped[m] = pair_pool.tile([P, STRETCH, PACK], BF16, name="w2_grouped", tag="w2_grouped", align_bytes=64)
+            nc.scalar.copy(
+                out=w2_grouped[m][:].rearrange("p w t -> p (w t)").bitcast(F32).rearrange(
+                    "p (e b r u) -> p e b r u", e=2, b=SETS, u=2
+                ),
+                in_=w2_turned[m][:].rearrange("p (u b r e) -> p e b r u", b=SETS, u=2, e=2),
+            )
+
+        def quantise_w2(m):
+            nc.vector.quantize_mx(
+                out=w2_codes[:, m, :].bitcast(FP8X4),
+                scales=w2_scales[:, m, :],
+                in_=w2_grouped[m][:].rearrange("p w t -> p (w t)"),
+            )
 
         accs = {}
         hidden = {}
@@ -282,10 +289,12 @@ def tile_parallelnca_pa_kernel(tc, x, w1, b1, w2, b2, out):
 
         def second_product(m, t, lo=0, hi=COLS):
             accs[m, t, lo] = new_bank(m == GROUPS - 1)
+            u, e = divmod(t, 2)
+            columns = slice(P * (2 * e + u), P * (2 * e + u + 1))
             nc.tensor.matmul_mx(
                 out=accs[m, t, lo][:, 0 : hi - lo],
-                lhsT=w2_codes[:, m, P * t : P * (t + 1)].bitcast(FP8X4),
-                lhsT_scale=w2_scales[:, m, P * t : P * (t + 1)],
+                lhsT=w2_codes[:, m, columns].bitcast(FP8X4),
+                lhsT_scale=w2_scales[:, m, columns],
                 rhs=hidden_codes[m, lo][:, 0 : hi - lo].bitcast(FP8X4),
                 rhs_scale=hidden_scales[m, lo][:, 0 : hi - lo],
                 start=True,
@@ -350,6 +359,7 @@ def tile_parallelnca_pa_kernel(tc, x, w1, b1, w2, b2, out):
         shifted = [j for j in range(NS) if shift_of(0, j)[1] != 0]
         transpose_unit(0)
         load_unit(RAW_BUFS)
+        load_w2(0)
         pad_x_scales()
         quantise_w1(0, 0, 4)
         shift_words(-1, 0, GROUPS)
@@ -382,6 +392,13 @@ def tile_parallelnca_pa_kernel(tc, x, w1, b1, w2, b2, out):
         for k in range(2, UNITS - 2):
             m, t = divmod(k, TILES)
             turned = turned_in(k)
+            if k % TILES == 2 and m + 1 < GROUPS:
+                load_w2(m + 1)
+            turned_now = k % TILES == (2 if m == 0 else 1)
+            if turned_now:
+                turn_w2(m)
+            if k % TILES == (3 if m == 0 else 2):
+                quantise_w2(m)
             before = NS - 1 if len(turned) == 2 else NS // 2
             first_passes(k, range(before), True, False)
             for i in turned:
@@ -393,6 +410,8 @@ def tile_parallelnca_pa_kernel(tc, x, w1, b1, w2, b2, out):
             first_passes(k, range(before, NS), False, True)
             for lo, hi in pieces_of(m):
                 activate(k, lo, hi)
+            if turned_now:
+                regroup_w2(m)
             if m > 0:
                 second_product(m - 1, t)
                 finish(m - 1, t)
@@ -414,6 +433,7 @@ def tile_parallelnca_pa_kernel(tc, x, w1, b1, w2, b2, out):
 
         second_product(last - 1, TILES - 2)
         finish(last - 1, TILES - 2)
+        quantise_w2(last)
         end_passes(ends[0], *long)
         second_product(last - 1, TILES - 1)
         finish(last - 1, TILES - 1)

@@ -183,8 +183,8 @@ def tile_parallelnca_pa_kernel(tc, x, w1, b1, w2, b2, out):
 
         def load_w2(m):
             w2_raw[m] = pair_pool.tile([P, 2, SETS, 2 * QUAD], BF16, name="w2_raw", tag="w2_raw", align_bytes=64)
-            for q in range(QUADS):
-                for u in range(2):
+            for u in range(2):
+                for q in (0, 2, 1, 3):
                     nc.sync.dma_start(
                         out=w2_raw[m][QUAD * q : QUAD * (q + 1), u], in_=w2_runs[m, q, u]
                     )

@@ -34,6 +34,13 @@ QUAD = 32
 QUADS = P // QUAD
 SETS = STRETCH // QUAD
 
+
+def w2_tiles(k):
+    return {4: [0, 1], 5: [2, 3]}.get(k, [])
+
+
+MAX_BLOCKS = NS + 2
+
 FLOPS = 2 * COLS * GROUPS * STRETCH * (NS * STRETCH + STRETCH)
 
 
@@ -42,6 +49,7 @@ def tile_parallelnca_pa_kernel(tc, x, w1, b1, w2, b2, out):
 
     x_rows = x.rearrange("n (g u q e) h w -> g n q u (e h w)", g=GROUPS, u=2, e=2)
     w1_rows = w1.rearrange("m (u p e) k -> m u e p k", u=2, e=2)
+    w2_rows = w2.rearrange("m (u p e) k -> m p u (e k)", u=2, e=2)
     w2_runs = w2.rearrange("m (b f) (u q k) -> m q u f b k", f=QUAD, u=2, q=QUADS)
     out_rows = out.rearrange("n (m u p e) h w -> m u p n (e h w)", m=GROUPS, u=2, e=2)
 
@@ -133,6 +141,7 @@ def tile_parallelnca_pa_kernel(tc, x, w1, b1, w2, b2, out):
         w1_raw = {}
         w2_raw = {}
         w2_turned = {}
+        w2_first = keep.tile([P, TILES, STRETCH], BF16, name="w2_first")
         w2_grouped = {}
         w_grouped = {}
         w1_codes = {}
@@ -149,8 +158,10 @@ def tile_parallelnca_pa_kernel(tc, x, w1, b1, w2, b2, out):
         def transpose_unit(k, helped=False):
             words = w1_raw[k][:].bitcast(F32)
             blocks = [words[:, WORDS * j : WORDS * (j + 1)] for j in range(NS)]
+            for t in w2_tiles(k):
+                blocks.append(w2_first[:, t, :].bitcast(F32))
             w_grouped[k] = pair_pool.tile(
-                [P, NS * STRETCH], BF16, name="w_grouped", tag="w_grouped", align_bytes=64
+                [P, MAX_BLOCKS * STRETCH], BF16, name="w_grouped", tag="w_grouped", align_bytes=64
             )
             grouped_words = w_grouped[k][:].bitcast(F32).rearrange("p (b r u) -> p b r u", r=P, u=2)
             for first in range(0, len(blocks), 2):
@@ -180,6 +191,16 @@ def tile_parallelnca_pa_kernel(tc, x, w1, b1, w2, b2, out):
         def quantise_unit(k):
             quantise_w1(k, 0, NS - 1)
             quantise_w1(k, NS - 1, NS)
+            tiles = w2_tiles(k)
+            if tiles:
+                for i, t in enumerate(tiles):
+                    u, e = divmod(t, 2)
+                    columns = slice(P * (2 * e + u), P * (2 * e + u + 1))
+                    nc.vector.quantize_mx(
+                        out=w2_codes[:, 0, columns].bitcast(FP8X4),
+                        scales=w2_scales[:, 0, columns],
+                        in_=w_grouped[k][:, STRETCH * (NS + i) : STRETCH * (NS + i + 1)],
+                    )
 
         def load_w2(m):
             w2_raw[m] = pair_pool.tile([P, 2, SETS, 2 * QUAD], BF16, name="w2_raw", tag="w2_raw", align_bytes=64)
@@ -359,7 +380,7 @@ def tile_parallelnca_pa_kernel(tc, x, w1, b1, w2, b2, out):
         shifted = [j for j in range(NS) if shift_of(0, j)[1] != 0]
         transpose_unit(0)
         load_unit(RAW_BUFS)
-        load_w2(0)
+        nc.sync.dma_start(out=w2_first[:].rearrange("p (u e) k -> p u (e k)", u=2), in_=w2_rows[0])
         pad_x_scales()
         quantise_w1(0, 0, 4)
         shift_words(-1, 0, GROUPS)
@@ -394,10 +415,10 @@ def tile_parallelnca_pa_kernel(tc, x, w1, b1, w2, b2, out):
             turned = turned_in(k)
             if k % TILES == 2 and m + 1 < GROUPS:
                 load_w2(m + 1)
-            turned_now = k % TILES == (2 if m == 0 else 1)
+            turned_now = k % TILES == 1
             if turned_now:
                 turn_w2(m)
-            if k % TILES == (3 if m == 0 else 2):
+            if k % TILES == 2 and m > 0:
                 quantise_w2(m)
             before = NS - 1 if len(turned) == 2 else NS // 2
             first_passes(k, range(before), True, False)

@@ -11,6 +11,7 @@ U8 = mybir.dt.uint8
 FP8X4 = mybir.dt.float8_e4m3fn_x4
 ADD = mybir.AluOpType.add
 RELU = mybir.ActivationFunctionType.Relu
+IDENTITY = mybir.ActivationFunctionType.Identity
 
 P = 128
 PACK = 4
@@ -72,6 +73,7 @@ def tile_parallelnca_pa_kernel(tc, x, w1, b1, w2, b2, out):
         x_codes = keep.tile([P, 3, GROUPS, PADDED], U32, name="x_codes", align_bytes=64)
         x_scales = keep.tile([P, 3, COLS], U8, name="x_scales", align_bytes=64)
         x_scales_padded = keep.tile([P, 3, PADDED], U8, name="x_scales_padded", align_bytes=64)
+        x_biased = keep.tile([P, PACK, BATCH, PIXELS], F32, name="x_biased")
         w2_codes = keep.tile([P, GROUPS, STRETCH], U32, name="w2_codes", align_bytes=64)
         w2_scales = keep.tile([P, GROUPS, STRETCH], U8, name="w2_scales", align_bytes=64)
 
@@ -292,10 +294,10 @@ def tile_parallelnca_pa_kernel(tc, x, w1, b1, w2, b2, out):
                 scale=1.0,
             )
 
-        def quantise_hidden(m, lo=0, hi=COLS):
+        def quantise_hidden(m, lo=0, hi=COLS, copy=nc.vector.tensor_copy):
             width = hi - lo
             grouped = pair_pool.tile([P, COLS, PACK], BF16, tag="hidden_grouped", align_bytes=64)
-            nc.vector.tensor_copy(
+            copy(
                 out=grouped[:, 0:width].rearrange("p (c i) t -> p c t i", i=4),
                 in_=hidden_piece(m, lo, hi).rearrange("p t (c i) -> p c t i", i=4),
             )
@@ -349,6 +351,16 @@ def tile_parallelnca_pa_kernel(tc, x, w1, b1, w2, b2, out):
                             out=out_rows[m, u, :, n].rearrange("p (e f) -> p e f", e=2)[:, :, first : first + span],
                             in_=out_tile[:, n],
                         )
+
+        def bias_x(t):
+            column = UNITS + TILES * (GROUPS - 1) + t
+            nc.scalar.activation(
+                out=x_biased[:, t],
+                in_=x_raw[:, :, GROUPS - 1, t, :],
+                func=IDENTITY,
+                bias=bias[:, column : column + 1],
+                scale=1.0,
+            )
 
         for g in range(GROUPS):
             load_x(g)
@@ -436,6 +448,8 @@ def tile_parallelnca_pa_kernel(tc, x, w1, b1, w2, b2, out):
             if m > 0:
                 second_product(m - 1, t)
                 finish(m - 1, t)
+            if m == 2:
+                bias_x(t)
             if t == TILES - 1:
                 quantise_hidden(m)
 
@@ -447,10 +461,41 @@ def tile_parallelnca_pa_kernel(tc, x, w1, b1, w2, b2, out):
             first_passes(k, range(NS), True, True, lo, hi)
             activate(k, lo, hi, lo)
 
-        def end_products(lo, hi):
-            for t in range(TILES):
-                second_product(last, t, lo, hi)
-                finish(last, t, lo, hi)
+        def end_products(lo, hi, per_bank):
+            width = hi - lo
+            pixels = slice(lo // BATCH, hi // BATCH)
+            span = PIXELS // 2
+            first = pixels.start - pixels.start % span
+            if first not in out_tiles:
+                out_tiles[first] = out_pool.tile([P, TILES, BATCH, span], F32, name="end_tile", tag="out_tile")
+            codes, scales = hidden_codes[last, lo], hidden_scales[last, lo]
+            for t0 in range(0, TILES, per_bank):
+                bank = turn_psum.tile([P, per_bank, width], F32, name="end_bank", tag="turned")
+                for t in range(t0, t0 + per_bank):
+                    u, e = divmod(t, 2)
+                    columns = slice(P * (2 * e + u), P * (2 * e + u + 1))
+                    nc.tensor.matmul_mx(
+                        out=bank[:, t - t0],
+                        lhsT=w2_codes[:, last, columns].bitcast(FP8X4),
+                        lhsT_scale=w2_scales[:, last, columns],
+                        rhs=codes[:, 0:width].bitcast(FP8X4),
+                        rhs_scale=scales[:, 0:width],
+                        start=True,
+                        stop=True,
+                    )
+                nc.vector.tensor_tensor(
+                    out=out_tiles[first][:, t0 : t0 + per_bank, :, pixels.start - first : pixels.stop - first],
+                    in0=bank[:].rearrange("p t (n f) -> p t n f", n=BATCH),
+                    in1=x_biased[:, t0 : t0 + per_bank, :, pixels],
+                    op=ADD,
+                )
+                if pixels.stop == first + span:
+                    for u in range(t0 // 2, (t0 + per_bank) // 2):
+                        for n in range(BATCH):
+                            nc.sync.dma_start(
+                                out=out_rows[last, u, :, n].rearrange("p (e f) -> p e f", e=2)[:, :, first : first + span],
+                                in_=out_tiles[first][:, 2 * u : 2 * u + 2, n],
+                            )
 
         second_product(last - 1, TILES - 2)
         finish(last - 1, TILES - 2)
@@ -464,8 +509,8 @@ def tile_parallelnca_pa_kernel(tc, x, w1, b1, w2, b2, out):
             end_passes(k, *middle)
         quantise_hidden(last, *middle)
         end_passes(ends[0], *short)
-        end_products(*long)
+        end_products(*long, 2)
         end_passes(ends[1], *short)
         quantise_hidden(last, *short)
-        end_products(*middle)
-        end_products(*short)
+        end_products(*middle, 4)
+        end_products(*short, 2)

@@ -432,12 +432,17 @@ def tile_parallelnca_pa_kernel(tc, x, w1, b1, w2, b2, out):
                 turn_w2(m)
             if k % TILES == 2 and m > 0:
                 quantise_w2(m)
-            before = NS - 1 if len(turned) == 2 else NS // 2
-            first_passes(k, range(before), True, False)
-            for i in turned:
+            stops = (4, 8) if len(turned) == 2 else (NS // 2,)
+            before = 0
+            for i, stop in zip(turned, stops):
+                first_passes(k, range(before, stop), before == 0, False)
+                before = stop
                 transpose_unit(i, helped=i < turned[-1])
                 if i + RAW_BUFS < UNITS:
                     load_unit(i + RAW_BUFS)
+            if not turned:
+                before = NS // 2
+                first_passes(k, range(before), True, False)
             if k + AHEAD < UNITS:
                 quantise_unit(k + AHEAD)
             first_passes(k, range(before, NS), False, True)

@@ -157,7 +157,7 @@ def tile_parallelnca_pa_kernel(tc, x, w1, b1, w2, b2, out):
             for lo in range(0, NS * STRETCH, width):
                 nc.sync.dma_start(out=w1_raw[k][:, lo : lo + width], in_=w1_rows[m, u, e, :, lo : lo + width])
 
-        def transpose_unit(k, helped=False):
+        def transpose_unit(k, helped=False, after_bank=None):
             words = w1_raw[k][:].bitcast(F32)
             blocks = [words[:, WORDS * j : WORDS * (j + 1)] for j in range(NS)]
             for t in w2_tiles(k):
@@ -179,6 +179,8 @@ def tile_parallelnca_pa_kernel(tc, x, w1, b1, w2, b2, out):
                     out=grouped_words[:, first : first + count],
                     in_=bank[:, 0:count].rearrange("p a u r -> p a r u"),
                 )
+                if after_bank is not None:
+                    after_bank(first)
 
         def quantise_w1(k, lo, hi):
             if k not in w1_codes:
@@ -371,16 +373,19 @@ def tile_parallelnca_pa_kernel(tc, x, w1, b1, w2, b2, out):
         for k in range(2, RAW_BUFS):
             load_unit(k)
 
-        idle_bank = turn_psum.tile([P, COLS], F32, name="idle_bank", tag="turned")
+        def keep_warm(g, n):
+            idle_bank = acc_psum.tile([P, COLS], F32, name="idle_bank", tag="acc")
+            nc.tensor.matmul(
+                idle_bank[:],
+                idle[:],
+                x_raw[:, n, g, 0:2].rearrange("q e f -> q (e f)"),
+                start=True,
+                stop=True,
+            )
+
         for g in range(GROUPS):
             for n in range(BATCH):
-                nc.tensor.matmul(
-                    idle_bank[:],
-                    idle[:],
-                    x_raw[:, n, g, 0:2].rearrange("q e f -> q (e f)"),
-                    start=True,
-                    stop=True,
-                )
+                keep_warm(g, n)
 
         for g in range(GROUPS + 1):
             if g < GROUPS:
@@ -390,7 +395,7 @@ def tile_parallelnca_pa_kernel(tc, x, w1, b1, w2, b2, out):
 
         unshifted = [j for j in range(NS) if shift_of(0, j)[1] == 0]
         shifted = [j for j in range(NS) if shift_of(0, j)[1] != 0]
-        transpose_unit(0)
+        transpose_unit(0, after_bank=lambda first: keep_warm(0, 0))
         load_unit(RAW_BUFS)
         nc.sync.dma_start(out=w2_first[:].rearrange("p (u e) k -> p u (e k)", u=2), in_=w2_rows[0])
         pad_x_scales()
@@ -437,7 +442,7 @@ def tile_parallelnca_pa_kernel(tc, x, w1, b1, w2, b2, out):
             for i, stop in zip(turned, stops):
                 first_passes(k, range(before, stop), before == 0, False)
                 before = stop
-                transpose_unit(i, helped=i < turned[-1])
+                transpose_unit(i, helped=i < turned[-1], after_bank=lambda first: keep_warm(0, 0) if first in (4,) else None)
                 if i + RAW_BUFS < UNITS:
                     load_unit(i + RAW_BUFS)
             if not turned:

from contextlib import ExitStack

import concourse.mybir as mybir
from concourse.masks import make_identity

BF16 = mybir.dt.bfloat16
F32 = mybir.dt.float32
I32 = mybir.dt.int32
U32 = mybir.dt.uint32
U8 = mybir.dt.uint8
FP8X4 = mybir.dt.float8_e4m3fn_x4
ADD = mybir.AluOpType.add
RELU = mybir.ActivationFunctionType.Relu
IDENTITY = mybir.ActivationFunctionType.Identity

P = 128
PACK = 4
STRETCH = P * PACK
WORDS = STRETCH // 2

BATCH, GROUPS, GRID = 2, 4, 16
LIVE = 4
PIXELS = GRID * GRID
COLS = BATCH * PIXELS
ROW = BATCH * GRID
PADDED = COLS + 2 * ROW
SHIFTS = [(0, 0)] + [(r, c) for r in (-1, 0, 1) for c in (-1, 0, 1) if (r, c) != (0, 0)]
NS = len(SHIFTS)
TILES = STRETCH // P
UNITS = GROUPS * TILES
BANKS = 5
AHEAD = 2
RAW_BUFS = 4
QUAD = 32
QUADS = P // QUAD
SETS = STRETCH // QUAD


def w2_tiles(k):
    return {4: [0, 1], 5: [2, 3]}.get(k, [])


MAX_BLOCKS = NS + 2

FLOPS = 2 * COLS * GROUPS * STRETCH * (NS * STRETCH + STRETCH)


def tile_parallelnca_pa_kernel(tc, x, w1, b1, w2, b2, out):
    nc = tc.nc

    x_rows = x.rearrange("n (g u q e) h w -> g n q u (e h w)", g=GROUPS, u=2, e=2)
    w1_rows = w1.rearrange("m (u p e) k -> m u e p k", u=2, e=2)
    w2_rows = w2.rearrange("m (u p e) k -> m p u (e k)", u=2, e=2)
    w2_runs = w2.rearrange("m (b f) (u q k) -> m q u f b k", f=QUAD, u=2, q=QUADS)
    out_rows = out.rearrange("n (m u p e) h w -> m u p n (e h w)", m=GROUPS, u=2, e=2)

    with ExitStack() as ctx:
        keep = ctx.enter_context(tc.tile_pool(name="keep", bufs=1))
        raw_pool = ctx.enter_context(tc.tile_pool(name="raw_pool", bufs=RAW_BUFS))
        pair_pool = ctx.enter_context(tc.tile_pool(name="pair_pool", bufs=2))
        code_pool = ctx.enter_context(tc.tile_pool(name="code_pool", bufs=AHEAD + 2))
        out_pool = ctx.enter_context(tc.tile_pool(name="out_pool", bufs=4))
        turn_psum = ctx.enter_context(tc.psum_pool(name="turn_psum", bufs=BANKS))
        acc_psum = ctx.enter_context(tc.psum_pool(name="acc_psum", bufs=3))
        ctx.enter_context(tc.manual_schedule())

        identity = keep.tile([P, P], F32, name="identity")
        idle = keep.tile([P, P], BF16, name="idle")
        bias_rows = keep.tile([P, 2 * P], BF16, name="bias_rows")
        bias = keep.tile([P, 2 * UNITS], F32, name="bias")
        x_raw = keep.tile([P, BATCH, GROUPS, PACK, PIXELS], BF16, name="x_raw")
        x_centre = keep.tile([P, GROUPS, GRID * BATCH, GRID, PACK], BF16, name="x_centre", align_bytes=64)
        x_codes = keep.tile([P, 3, GROUPS, PADDED], U32, name="x_codes", align_bytes=64)
        x_scales = keep.tile([P, 3, COLS], U8, name="x_scales", align_bytes=64)
        x_scales_padded = keep.tile([P, 3, PADDED], U8, name="x_scales_padded", align_bytes=64)
        x_biased = keep.tile([P, PACK, BATCH, PIXELS], F32, name="x_biased")
        w2_codes = keep.tile([P, GROUPS, STRETCH], U32, name="w2_codes", align_bytes=64)
        w2_scales = keep.tile([P, GROUPS, STRETCH], U8, name="w2_scales", align_bytes=64)

        def x_words(c, lo, hi):
            words = x_codes[:, c + 1, lo:hi, ROW : ROW + COLS].bitcast(I32)
            return words.rearrange("q g (a j) -> q g a j", j=GRID)

        nc.gpsimd.memset(idle[:], 0.0)
        nc.gpsimd.memset(x_scales[:, 1].bitcast(I32), 0)
        nc.gpsimd.memset(bias_rows[:], 0.0)
        make_identity(nc, identity[:])
        nc.vector.memset(x_scales_padded[:, :, 0 : ROW + 4].bitcast(I32), 0)
        nc.vector.memset(x_scales_padded[:, :, ROW + COLS - 4 : PADDED].bitcast(I32), 0)
        nc.vector.memset(x_codes[:, :, :, 0:ROW].bitcast(I32), 0)
        nc.vector.memset(x_codes[:, :, :, ROW + COLS : PADDED].bitcast(I32), 0)
        for c in (-1, 1):
            border = 0 if c < 0 else GRID - 1
            nc.vector.memset(x_words(c, 0, GROUPS)[:, :, :, border], 0)

        def load_x(g):
            for n, queue in ((0, nc.sync), (1, nc.scalar)):
                queue.dma_start(
                    out=x_raw[:, n, g].rearrange("q (u e) f -> q u (e f)", u=2),
                    in_=x_rows[g, n],
                )

        def regroup_x(g):
            grouped = x_centre[:, g].rearrange("q (i n) j t -> q i n j t", n=BATCH)
            for n, copy in ((0, nc.vector.tensor_copy), (1, nc.scalar.copy)):
                copy(
                    out=grouped[:, :, n].rearrange("q i (c s) t -> q i c t s", s=4),
                    in_=x_raw[:, n, g].rearrange("q t (i c s) -> q i c t s", c=GRID // 4, s=4),
                )

        def quantise_x(g):
            nc.vector.quantize_mx(
                out=x_codes[:, 1, g, ROW : ROW + COLS].bitcast(FP8X4),
                scales=x_scales[LIVE * g : P, 1, :],
                in_=x_centre[:, g].rearrange("q a j t -> q (a j t)"),
            )

        def shift_words(c, lo, hi):
            first, last = max(0, -c), GRID - max(0, c)
            nc.vector.tensor_copy(
                out=x_words(c, lo, hi)[:, :, :, first:last],
                in_=x_words(0, lo, hi)[:, :, :, first + c : last + c],
            )

        def shift_scales(c):
            nc.vector.tensor_copy(
                out=x_scales_padded[:, c + 1, ROW - c : ROW - c + COLS],
                in_=x_scales[:, 1],
            )

        def pad_x_scales():
            nc.vector.tensor_copy(
                out=x_scales_padded[:, 1, ROW : ROW + COLS].bitcast(I32),
                in_=x_scales[:, 1].bitcast(I32),
            )

        def unpad_x_scales(c):
            nc.vector.tensor_copy(
                out=x_scales[:, c + 1].bitcast(I32),
                in_=x_scales_padded[:, c + 1, ROW : ROW + COLS].bitcast(I32),
            )

        w1_raw = {}
        w2_raw = {}
        w2_turned = {}
        w2_first = keep.tile([P, TILES, STRETCH], BF16, name="w2_first")
        w2_grouped = {}
        w_grouped = {}
        w1_codes = {}
        w1_scales = {}

        def load_unit(k, pieces=1):
            m, t = divmod(k, TILES)
            u, e = divmod(t, 2)
            w1_raw[k] = raw_pool.tile([P, NS * STRETCH], BF16, name="w1_raw", tag="w1_raw")
            width = NS * STRETCH // pieces
            for lo in range(0, NS * STRETCH, width):
                nc.sync.dma_start(out=w1_raw[k][:, lo : lo + width], in_=w1_rows[m, u, e, :, lo : lo + width])

        def transpose_unit(k, helped=False, after_bank=None):
            words = w1_raw[k][:].bitcast(F32)
            blocks = [words[:, WORDS * j : WORDS * (j + 1)] for j in range(NS)]
            for t in w2_tiles(k):
                blocks.append(w2_first[:, t, :].bitcast(F32))
            w_grouped[k] = pair_pool.tile(
                [P, MAX_BLOCKS * STRETCH], BF16, name="w_grouped", tag="w_grouped", align_bytes=64
            )
            grouped_words = w_grouped[k][:].bitcast(F32).rearrange("p (b r u) -> p b r u", r=P, u=2)
            for first in range(0, len(blocks), 2):
                count = min(2, len(blocks) - first)
                bank = turn_psum.tile([P, 2, 2, P], F32, tag="turned")
                for a in range(count):
                    for u in range(2):
                        nc.tensor.transpose(
                            bank[:, a, u, :], blocks[first + a][:, P * u : P * (u + 1)], identity[:]
                        )
                copy = nc.vector.tensor_copy if helped and first // 2 % 2 else nc.scalar.copy
                copy(
                    out=grouped_words[:, first : first + count],
                    in_=bank[:, 0:count].rearrange("p a u r -> p a r u"),
                )
                if after_bank is not None:
                    after_bank(first)

        def quantise_w1(k, lo, hi):
            if k not in w1_codes:
                w1_codes[k] = code_pool.tile([P, NS * P], U32, name="w1_codes", tag="w1_codes", align_bytes=64)
                w1_scales[k] = code_pool.tile([P, NS * P], U8, name="w1_scales", tag="w1_scales", align_bytes=64)
            nc.vector.quantize_mx(
                out=w1_codes[k][:, P * lo : P * hi].bitcast(FP8X4),
                scales=w1_scales[k][:, P * lo : P * hi],
                in_=w_grouped[k][:, STRETCH * lo : STRETCH * hi],
            )

        def quantise_unit(k):
            quantise_w1(k, 0, NS - 1)
            quantise_w1(k, NS - 1, NS)
            tiles = w2_tiles(k)
            if tiles:
                for i, t in enumerate(tiles):
                    u, e = divmod(t, 2)
                    columns = slice(P * (2 * e + u), P * (2 * e + u + 1))
                    nc.vector.quantize_mx(
                        out=w2_codes[:, 0, columns].bitcast(FP8X4),
                        scales=w2_scales[:, 0, columns],
                        in_=w_grouped[k][:, STRETCH * (NS + i) : STRETCH * (NS + i + 1)],
                    )

        def load_w2(m):
            w2_raw[m] = pair_pool.tile([P, 2, SETS, 2 * QUAD], BF16, name="w2_raw", tag="w2_raw", align_bytes=64)
            for u in range(2):
                for q in (0, 2, 1, 3):
                    nc.sync.dma_start(
                        out=w2_raw[m][QUAD * q : QUAD * (q + 1), u], in_=w2_runs[m, q, u]
                    )

        def turn_w2(m):
            w2_turned[m] = pair_pool.tile([P, SETS * 2 * QUAD], F32, name="w2_turned", tag="w2_turned", align_bytes=64)
            nc.vector.transpose(w2_turned[m][:], w2_raw[m][:].rearrange("p u b k -> p (u b k)").bitcast(F32))

        def regroup_w2(m):
            w2_grouped[m] = pair_pool.tile([P, STRETCH, PACK], BF16, name="w2_grouped", tag="w2_grouped", align_bytes=64)
            nc.scalar.copy(
                out=w2_grouped[m][:].rearrange("p w t -> p (w t)").bitcast(F32).rearrange(
                    "p (e b r u) -> p e b r u", e=2, b=SETS, u=2
                ),
                in_=w2_turned[m][:].rearrange("p (u b r e) -> p e b r u", b=SETS, u=2, e=2),
            )

        def quantise_w2(m):
            nc.vector.quantize_mx(
                out=w2_codes[:, m, :].bitcast(FP8X4),
                scales=w2_scales[:, m, :],
                in_=w2_grouped[m][:].rearrange("p w t -> p (w t)"),
            )

        accs = {}
        hidden = {}
        hidden_codes = {}
        hidden_scales = {}
        out_tiles = {}

        def shift_of(m, j):
            copy_number, g = divmod(m * NS + j, GROUPS)
            return SHIFTS[copy_number] + (g,)

        def turned_in(k):
            if k < TILES:
                return [k + AHEAD]
            return [i for i in (k + AHEAD, k + AHEAD + 1) if k % 2 == 0 and i < UNITS]

        def pieces_of(m):
            half, quarter = COLS // 2, COLS // 4
            if m == GROUPS - 1:
                return [(0, half), (half, COLS - quarter), (COLS - quarter, COLS)]
            return [(0, COLS)]

        def new_bank(at_end):
            if at_end:
                return turn_psum.tile([P, COLS], F32, name="acc", tag="turned")
            return acc_psum.tile([P, COLS], F32, name="acc", tag="acc")

        def first_passes(k, passes, start, stop, lo=0, hi=COLS):
            m = k // TILES
            if start:
                accs[k, lo] = new_bank(k >= UNITS - 2)
            for j in passes:
                r, c, g = shift_of(m, j)
                window = slice(ROW * (1 + r) + lo, ROW * (1 + r) + hi)
                if r == 0:
                    rhs_scale = x_scales[LIVE * g : P, c + 1, lo:hi]
                else:
                    rhs_scale = x_scales_padded[LIVE * g : P, c + 1, window]
                nc.tensor.matmul_mx(
                    out=accs[k, lo][:, 0 : hi - lo],
                    lhsT=w1_codes[k][:, P * j : P * (j + 1)].bitcast(FP8X4),
                    lhsT_scale=w1_scales[k][:, P * j : P * (j + 1)],
                    rhs=x_codes[:, c + 1, g, window].bitcast(FP8X4),
                    rhs_scale=rhs_scale,
                    start=start and j == passes[0],
                    stop=stop and j == passes[-1],
                )

        def hidden_piece(m, lo, hi):
            return hidden[m][:, TILES * lo : TILES * hi].rearrange("p (t f) -> p t f", t=TILES)

        def activate(k, lo=0, hi=COLS, base=0):
            m, t = divmod(k, TILES)
            if m not in hidden:
                hidden[m] = pair_pool.tile([P, TILES * COLS], BF16, name="hidden", tag="hidden")
            nc.scalar.activation(
                out=hidden_piece(m, lo, hi)[:, t].rearrange("p (n i j) -> p n i j", n=BATCH, j=GRID),
                in_=accs[k, base][:, lo - base : hi - base].rearrange("p (i n j) -> p n i j", n=BATCH, j=GRID),
                func=RELU,
                bias=bias[:, k : k + 1],
                scale=1.0,
            )

        def quantise_hidden(m, lo=0, hi=COLS, copy=nc.vector.tensor_copy):
            width = hi - lo
            grouped = pair_pool.tile([P, COLS, PACK], BF16, tag="hidden_grouped", align_bytes=64)
            copy(
                out=grouped[:, 0:width].rearrange("p (c i) t -> p c t i", i=4),
                in_=hidden_piece(m, lo, hi).rearrange("p t (c i) -> p c t i", i=4),
            )
            codes = pair_pool.tile([P, COLS], U32, name="hidden_codes", tag="hidden_codes", align_bytes=64)
            scales = pair_pool.tile([P, COLS], U8, name="hidden_scales", tag="hidden_scales", align_bytes=64)
            hidden_codes[m, lo], hidden_scales[m, lo] = codes, scales
            nc.vector.quantize_mx(
                out=codes[:, 0:width].bitcast(FP8X4),
                scales=scales[:, 0:width],
                in_=grouped[:, 0:width].rearrange("p w t -> p (w t)"),
            )

        def second_product(m, t, lo=0, hi=COLS):
            accs[m, t, lo] = new_bank(m == GROUPS - 1)
            u, e = divmod(t, 2)
            columns = slice(P * (2 * e + u), P * (2 * e + u + 1))
            nc.tensor.matmul_mx(
                out=accs[m, t, lo][:, 0 : hi - lo],
                lhsT=w2_codes[:, m, columns].bitcast(FP8X4),
                lhsT_scale=w2_scales[:, m, columns],
                rhs=hidden_codes[m, lo][:, 0 : hi - lo].bitcast(FP8X4),
                rhs_scale=hidden_scales[m, lo][:, 0 : hi - lo],
                start=True,
                stop=True,
            )

        def finish(m, t, lo=0, hi=COLS):
            u, e = divmod(t, 2)
            pixels = slice(lo // BATCH, hi // BATCH)
            span = PIXELS if m < GROUPS - 1 else PIXELS // 2
            first = pixels.start - pixels.start % span
            if (m, u, first) not in out_tiles:
                out_tiles[m, u, first] = out_pool.tile(
                    [P, BATCH, 2, span], F32, name="out_tile", tag="out_tile"
                )
            out_tile = out_tiles[m, u, first]
            nc.vector.scalar_tensor_tensor(
                out=out_tile[:, :, e, pixels.start - first : pixels.stop - first],
                in0=accs[m, t, lo][:, 0 : hi - lo].rearrange("p (n f) -> p n f", n=BATCH),
                scalar=bias[:, UNITS + TILES * m + t : UNITS + TILES * m + t + 1],
                in1=x_raw[:, :, m, t, pixels],
                op0=ADD,
                op1=ADD,
            )
            if e == 1 and pixels.stop == first + span:
                if span == PIXELS:
                    nc.sync.dma_start(out=out_rows[m, u], in_=out_tile[:].rearrange("p n e f -> p n (e f)"))
                else:
                    for n in range(BATCH):
                        nc.sync.dma_start(
                            out=out_rows[m, u, :, n].rearrange("p (e f) -> p e f", e=2)[:, :, first : first + span],
                            in_=out_tile[:, n],
                        )

        def bias_x(t):
            column = UNITS + TILES * (GROUPS - 1) + t
            nc.scalar.activation(
                out=x_biased[:, t],
                in_=x_raw[:, :, GROUPS - 1, t, :],
                func=IDENTITY,
                bias=bias[:, column : column + 1],
                scale=1.0,
            )

        for g in range(GROUPS):
            load_x(g)
        load_unit(0, pieces=3)
        nc.sync.dma_start(out=bias_rows[0:8, :], in_=b1.rearrange("(r c) -> r c", c=2 * P))
        nc.sync.dma_start(out=bias_rows[8:16, :], in_=b2.rearrange("(r c) -> r c", c=2 * P))
        load_unit(1, pieces=3)
        for k in range(2, RAW_BUFS):
            load_unit(k)

        def keep_warm(g, n):
            idle_bank = acc_psum.tile([P, COLS], F32, name="idle_bank", tag="acc")
            nc.tensor.matmul(
                idle_bank[:],
                idle[:],
                x_raw[:, n, g, 0:2].rearrange("q e f -> q (e f)"),
                start=True,
                stop=True,
            )

        for g in range(GROUPS):
            for n in range(BATCH):
                keep_warm(g, n)

        for g in range(GROUPS + 1):
            if g < GROUPS:
                regroup_x(g)
            if g > 0:
                quantise_x(g - 1)

        unshifted = [j for j in range(NS) if shift_of(0, j)[1] == 0]
        shifted = [j for j in range(NS) if shift_of(0, j)[1] != 0]
        transpose_unit(0, after_bank=lambda first: keep_warm(0, 0))
        load_unit(RAW_BUFS)
        nc.sync.dma_start(out=w2_first[:].rearrange("p (u e) k -> p u (e k)", u=2), in_=w2_rows[0])
        pad_x_scales()
        quantise_w1(0, 0, 4)
        shift_words(-1, 0, GROUPS)
        quantise_w1(0, NS - 1, NS)
        shift_scales(-1)
        quantise_w1(0, 4, NS - 1)
        first_passes(0, unshifted, True, False)
        transpose_unit(1)
        load_unit(RAW_BUFS + 1)
        bias_bank = turn_psum.tile([P, 2, 2, P], F32, tag="turned")
        nc.tensor.transpose(bias_bank[:, 0, 0, :], bias_rows[:].bitcast(F32), identity[:])
        nc.vector.tensor_copy(out=bias[:], in_=bias_bank[:, 0, 0, 0:UNITS].bitcast(BF16))
        first_passes(0, shifted, False, True)
        activate(0)
        quantise_unit(1)
        transpose_unit(2)
        load_unit(RAW_BUFS + 2)
        quantise_unit(2)
        shift_words(1, 0, 2)
        shift_scales(1)
        first_passes(1, range(NS), True, True)
        activate(1)
        transpose_unit(3)
        load_unit(RAW_BUFS + 3)
        quantise_unit(3)
        shift_words(1, 2, GROUPS)
        unpad_x_scales(-1)
        unpad_x_scales(1)

        for k in range(2, UNITS - 2):
            m, t = divmod(k, TILES)
            turned = turned_in(k)
            if k % TILES == 2 and m + 1 < GROUPS:
                load_w2(m + 1)
            turned_now = k % TILES == 1
            if turned_now:
                turn_w2(m)
            if k % TILES == 2 and m > 0:
                quantise_w2(m)
            stops = (4, 8) if len(turned) == 2 else (NS // 2,)
            before = 0
            for i, stop in zip(turned, stops):
                first_passes(k, range(before, stop), before == 0, False)
                before = stop
                transpose_unit(i, helped=i < turned[-1], after_bank=lambda first: keep_warm(0, 0) if first in (4,) else None)
                if i + RAW_BUFS < UNITS:
                    load_unit(i + RAW_BUFS)
            if not turned:
                before = NS // 2
                first_passes(k, range(before), True, False)
            if k + AHEAD < UNITS:
                quantise_unit(k + AHEAD)
            first_passes(k, range(before, NS), False, True)
            for lo, hi in pieces_of(m):
                activate(k, lo, hi)
            if turned_now:
                regroup_w2(m)
            if m > 0:
                second_product(m - 1, t)
                finish(m - 1, t)
            if m == 2:
                bias_x(t)
            if t == TILES - 1:
                quantise_hidden(m)

        last = GROUPS - 1
        ends = (UNITS - 2, UNITS - 1)
        long, middle, short = pieces_of(last)

        def end_passes(k, lo, hi):
            first_passes(k, range(NS), True, True, lo, hi)
            activate(k, lo, hi, lo)

        def end_products(lo, hi, per_bank):
            width = hi - lo
            pixels = slice(lo // BATCH, hi // BATCH)
            span = PIXELS // 2
            first = pixels.start - pixels.start % span
            if first not in out_tiles:
                out_tiles[first] = out_pool.tile([P, TILES, BATCH, span], F32, name="end_tile", tag="out_tile")
            codes, scales = hidden_codes[last, lo], hidden_scales[last, lo]
            for t0 in range(0, TILES, per_bank):
                bank = turn_psum.tile([P, per_bank, width], F32, name="end_bank", tag="turned")
                for t in range(t0, t0 + per_bank):
                    u, e = divmod(t, 2)
                    columns = slice(P * (2 * e + u), P * (2 * e + u + 1))
                    nc.tensor.matmul_mx(
                        out=bank[:, t - t0],
                        lhsT=w2_codes[:, last, columns].bitcast(FP8X4),
                        lhsT_scale=w2_scales[:, last, columns],
                        rhs=codes[:, 0:width].bitcast(FP8X4),
                        rhs_scale=scales[:, 0:width],
                        start=True,
                        stop=True,
                    )
                nc.vector.tensor_tensor(
                    out=out_tiles[first][:, t0 : t0 + per_bank, :, pixels.start - first : pixels.stop - first],
                    in0=bank[:].rearrange("p t (n f) -> p t n f", n=BATCH),
                    in1=x_biased[:, t0 : t0 + per_bank, :, pixels],
                    op=ADD,
                )
                if pixels.stop == first + span:
                    for u in range(t0 // 2, (t0 + per_bank) // 2):
                        for n in range(BATCH):
                            nc.sync.dma_start(
                                out=out_rows[last, u, :, n].rearrange("p (e f) -> p e f", e=2)[:, :, first : first + span],
                                in_=out_tiles[first][:, 2 * u : 2 * u + 2, n],
                            )

        second_product(last - 1, TILES - 2)
        finish(last - 1, TILES - 2)
        quantise_w2(last)
        end_passes(ends[0], *long)
        second_product(last - 1, TILES - 1)
        finish(last - 1, TILES - 1)
        end_passes(ends[1], *long)
        quantise_hidden(last, *long)
        for k in ends:
            end_passes(k, *middle)
        quantise_hidden(last, *middle)
        end_passes(ends[0], *short)
        end_products(*long, 2)
        end_passes(ends[1], *short)
        quantise_hidden(last, *short)
        end_products(*middle, 4)
        end_products(*short, 2)
